import numpy as np
import ml_dtypes


def mxq(x, axis, fmt="e4m3"):
    dtype, down = {"e4m3": (ml_dtypes.float8_e4m3fn, 7), "e5m2": (ml_dtypes.float8_e5m2, 14)}[fmt]
    v = np.moveaxis(np.asarray(x, np.float32).astype(ml_dtypes.bfloat16).astype(np.float64), axis, -1)
    blocks = v.reshape(v.shape[:-1] + (-1, 32))
    amax = np.abs(blocks).max(-1, keepdims=True)
    byte = np.maximum(np.where(amax > 0, np.frexp(amax)[1] - 1 + 127, 0) - down, 1)
    scale = np.exp2(byte - 127.0)
    codes = (blocks / scale).astype(np.float32).astype(dtype).astype(np.float64)
    return np.moveaxis((codes * scale).reshape(v.shape), -1, axis)


WIDE = False


def mx_kscale(k):
    if not WIDE:
        return np.ones(k)
    levels = np.array([10, -10, 5, -5, 0])
    a = np.random.permutation(np.resize(levels, k // 512 * 4)).reshape(k // 512, 4)
    idx = np.arange(k)
    return np.exp2(a[idx // 512, idx % 128 // 32])


BF16 = ml_dtypes.bfloat16


def bf(x):
    return np.asarray(x, np.float32).astype(BF16)


def f64(x):
    return np.asarray(x).astype(np.float64)


B, IN, HID, N, NM = 2, 128, 384, 512, 5
C = IN + HID
K = NM * C


def setup_inputs():
    t = mx_kscale(C)
    tc = t[None, :, None]
    return {"x_cand": bf(np.random.standard_normal((B, C, N)) * 0.8 * tc),
            "x1_0": bf(np.random.standard_normal((B, C, N)) * 0.55 * tc),
            "x1_1": bf(np.random.standard_normal((B, C, N)) * 0.55 * tc),
            "support0": bf(np.random.standard_normal((N, N)) * 0.7 / np.sqrt(N)),
            "support1": bf(np.random.standard_normal((N, N)) * 0.7 / np.sqrt(N)),
            "W_c": bf(np.random.standard_normal((K, HID)) / np.sqrt(K) / np.tile(t, NM)[:, None]),
            "b_c": bf(0.3 * np.random.standard_normal(HID)),
            "u": bf(1.0 / (1.0 + np.exp(-(1.0 + np.random.standard_normal((B, HID, N)))))),
            "hx": bf(np.random.standard_normal((B, HID, N)))}


def reference(x_cand, x1_0, x1_1, support0, support1, W_c, b_c, u, hx):
    x0, xa, xb = f64(x_cand), f64(x1_0), f64(x1_1)
    x2a = 2.0 * (mxq(xa, 2, "e4m3") @ mxq(f64(support0).T, 0, "e4m3")) - x0
    x2b = 2.0 * (mxq(xb, 2, "e4m3") @ mxq(f64(support1).T, 0, "e4m3")) - x0
    h = np.concatenate([x0, xa, x2a, xb, x2b], axis=1)
    cand = np.tanh((mxq(f64(W_c).T, 1, "e4m3") @ mxq(h, 1, "e4m3")) + f64(b_c)[None, :, None])
    return f64(u) * f64(hx) + (1.0 - f64(u)) * cand

@@ -1,0 +1,208 @@
+from contextlib import ExitStack
+
+import concourse.mybir as mybir
+from concourse.masks import make_identity
+
+BF16 = mybir.dt.bfloat16
+F32 = mybir.dt.float32
+U32 = mybir.dt.uint32
+U8 = mybir.dt.uint8
+FP8X4 = mybir.dt.float8_e4m3fn_x4
+ALU = mybir.AluOpType
+ACT = mybir.ActivationFunctionType
+
+P = 128
+PACK = 4
+BATCH = 2
+GRAPHS = 2
+CH = 512
+NODES = 512
+HID = 384
+HID_TILES = HID // P
+BLOCKS = 5
+X0, X1, X2 = 0, (1, 3), (2, 4)
+HALF = NODES // 2
+
+FLOPS = 2 * GRAPHS * BATCH * CH * NODES * NODES + 2 * BATCH * BLOCKS * CH * HID * NODES
+
+
+def tile_dcgrucell_pc_kernel(
+    tc, x_cand, x1_0, x1_1, support0, support1, W_c, b_c, u, hx, out
+):
+    nc = tc.nc
+    with ExitStack() as ctx:
+        const = ctx.enter_context(tc.tile_pool(name="const", bufs=1))
+        raw = ctx.enter_context(tc.tile_pool(name="raw", bufs=1))
+        side = ctx.enter_context(tc.tile_pool(name="side", bufs=6))
+        mx = ctx.enter_context(tc.tile_pool(name="mx", bufs=1))
+        gate = ctx.enter_context(tc.tile_pool(name="gate", bufs=3))
+        flip_psum = ctx.enter_context(tc.psum_pool(name="flip_psum", bufs=2))
+        step_psum = ctx.enter_context(tc.psum_pool(name="step_psum", bufs=3))
+        mix_psum = ctx.enter_context(tc.psum_pool(name="mix_psum", bufs=HID_TILES))
+
+        def load_channels(x, b, name):
+            rows = raw.tile([P, PACK * NODES], BF16, name=name)
+            nc.sync.dma_start(out=rows[:], in_=x[b].rearrange("(p j) n -> p (j n)", j=PACK))
+            return rows
+
+        def load_support(support, name):
+            rows = raw.tile([P, PACK * NODES], BF16, name=name)
+            nc.sync.dma_start(
+                out=rows[:].rearrange("p (a n) -> p a n", a=PACK),
+                in_=support.rearrange("(a p) n -> p a n", p=P),
+            )
+            return rows
+
+        x0_rows = [None] * BATCH
+        x1_rows = [[None] * BATCH for g in range(GRAPHS)]
+        s_rows = [None] * GRAPHS
+        s_rows[0] = load_support(support0, "s_rows0")
+        x1_rows[0][0] = load_channels(x1_0, 0, "x1_rows00")
+        x0_rows[0] = load_channels(x_cand, 0, "x0_rows0")
+        s_rows[1] = load_support(support1, "s_rows1")
+        x1_rows[1][0] = load_channels(x1_1, 0, "x1_rows10")
+        x1_rows[0][1] = load_channels(x1_0, 1, "x1_rows01")
+        x1_rows[1][1] = load_channels(x1_1, 1, "x1_rows11")
+        x0_rows[1] = load_channels(x_cand, 1, "x0_rows1")
+        w_rows = []
+        for i in range(BLOCKS):
+            rows = raw.tile([P, PACK * HID], BF16, name="w_rows%d" % i)
+            nc.sync.dma_start(
+                out=rows[:],
+                in_=W_c[i * CH : (i + 1) * CH, :].rearrange("(p j) o -> p (j o)", j=PACK),
+            )
+            w_rows.append(rows)
+        hx_rows = raw.tile([P, BATCH * HID_TILES, NODES], BF16, name="hx_rows")
+        nc.sync.dma_start(out=hx_rows[:], in_=hx.rearrange("b (a p) n -> p (b a) n", p=P))
+        u_rows = raw.tile([P, BATCH * HID_TILES, NODES], BF16, name="u_rows")
+        nc.sync.dma_start(out=u_rows[:], in_=u.rearrange("b (a p) n -> p (b a) n", p=P))
+
+        ident = const.tile([P, P], F32, name="ident")
+        make_identity(nc, ident[:])
+        bias_bf = const.tile([P, HID_TILES], BF16, name="bias_bf")
+        with nc.allow_non_contiguous_dma(reason="384 bias values, one to a partition and tile"):
+            nc.scalar.dma_start(out=bias_bf[:], in_=b_c.rearrange("(a p) -> p a", p=P))
+        bias = const.tile([P, HID_TILES], F32, name="bias")
+        nc.vector.tensor_copy(out=bias[:], in_=bias_bf[:])
+        warm = const.tile([P, 1], F32, name="warm")
+        nc.scalar.activation(out=warm[:], in_=ident[:, 0:1], func=ACT.Tanh)
+
+        def mx_operand(width, name):
+            codes = mx.tile([P, width], U32, name=name + "_codes", align_bytes=64)
+            scales = mx.tile([P, width], U8, name=name + "_scales", align_bytes=64)
+            return codes, scales
+
+        def quantise(operand, cols, values):
+            codes, scales = operand
+            nc.vector.quantize_mx(
+                out=codes[:, cols].bitcast(FP8X4), scales=scales[:, cols], in_=values
+            )
+
+        def mx_pass(acc, stationary, s_cols, moving, m_cols, start, stop):
+            nc.tensor.matmul_mx(
+                out=acc,
+                lhsT=stationary[0][:, s_cols].bitcast(FP8X4),
+                lhsT_scale=stationary[1][:, s_cols],
+                rhs=moving[0][:, m_cols].bitcast(FP8X4),
+                rhs_scale=moving[1][:, m_cols],
+                start=start,
+                stop=stop,
+            )
+
+        s_mx = [mx_operand(NODES, "s_mx%d" % g) for g in range(GRAPHS)]
+        x1_mx = [[mx_operand(CH, "x1_mx%d%d" % (g, b)) for b in range(BATCH)] for g in range(GRAPHS)]
+        h_mx = [[mx_operand(NODES, "h_mx%d%d" % (b, i)) for i in range(BLOCKS)] for b in range(BATCH)]
+        w_mx = [mx_operand(HID, "w_mx%d" % i) for i in range(BLOCKS)]
+
+        def nodes_to_partitions(rows, operand):
+            words = rows[:].bitcast(F32).rearrange("p (s w) -> p s w", s=PACK)
+            packed = side.tile([P, PACK * CH], BF16, name="packed", tag="side", align_bytes=64)
+            packed_words = packed[:].bitcast(F32).rearrange("p (c v) -> p c v", v=2)
+            for pair in range(2):
+                bank = flip_psum.tile([P, 2, 2 * P], F32, name="flip_bank")
+                for s in range(2):
+                    for v in range(2):
+                        nc.tensor.transpose(
+                            bank[:, v, s * P : (s + 1) * P],
+                            words[:, 2 * pair + s, v * P : (v + 1) * P],
+                            ident[:],
+                        )
+                nc.scalar.copy(
+                    out=packed_words[:, pair * 2 * P : (pair + 1) * 2 * P, :],
+                    in_=bank[:].rearrange("p v c -> p c v"),
+                )
+            quantise(operand, slice(0, CH), packed[:])
+
+        def channels_side_by_side(rows, width, operand, widths):
+            packed = side.tile([P, width * PACK], BF16, name="packed", tag="side", align_bytes=64)
+            nc.scalar.copy(
+                out=packed[:].rearrange("p (c i j) -> p c j i", i=4, j=PACK),
+                in_=rows[:].rearrange("p (j c i) -> p c j i", j=PACK, i=4),
+            )
+            first = 0
+            for w in widths:
+                quantise(operand, slice(first, first + w), packed[:, first * PACK : (first + w) * PACK])
+                first += w
+
+        def diffusion_step(g, b):
+            packed = side.tile([P, NODES * PACK], BF16, name="packed", tag="side", align_bytes=64)
+            packed_nj = packed[:].rearrange("p (n j) -> p n j", j=PACK)
+            x0_jn = x0_rows[b][:].rearrange("p (j n) -> p j n", j=PACK)
+            for r in range(NODES // P):
+                nodes = slice(r * P, (r + 1) * P)
+                bank = step_psum.tile([P, PACK, P], F32, name="step_bank")
+                for j in range(PACK):
+                    mx_pass(bank[:, j, :], x1_mx[g][b], slice(j * P, (j + 1) * P), s_mx[g], nodes, True, True)
+                nc.vector.scalar_tensor_tensor(
+                    out=packed_nj[:, nodes, :],
+                    in0=bank[:].rearrange("p j n -> p n j"),
+                    scalar=2.0,
+                    in1=x0_jn[:, :, nodes].rearrange("p j n -> p n j"),
+                    op0=ALU.mult,
+                    op1=ALU.subtract,
+                )
+            quantise(h_mx[b][X2[g]], slice(0, NODES), packed[:])
+
+        u_hx = const.tile([P, BATCH * HID_TILES, NODES], F32, name="u_hx")
+
+        def mix_channels(b, block_order):
+            tiles = slice(b * HID_TILES, (b + 1) * HID_TILES)
+            nc.vector.tensor_tensor(out=u_hx[:, tiles, :], in0=u_rows[:, tiles, :], in1=hx_rows[:, tiles, :], op=ALU.mult)
+            accs = [mix_psum.tile([P, NODES], F32, name="mix_acc") for a in range(HID_TILES)]
+            for k, i in enumerate(block_order):
+                for a in range(HID_TILES):
+                    mx_pass(accs[a][:], w_mx[i], slice(a * P, (a + 1) * P), h_mx[b][i], slice(0, NODES), k == 0, k == BLOCKS - 1)
+            for a in range(HID_TILES):
+                t = b * HID_TILES + a
+                cand = gate.tile([P, NODES], F32, name="cand")
+                nc.scalar.activation(out=cand[:], in_=accs[a][:], func=ACT.Tanh, bias=bias[:, a : a + 1], scale=1.0)
+                minus = gate.tile([P, NODES], F32, name="minus")
+                nc.vector.scalar_tensor_tensor(
+                    out=minus[:], in0=u_rows[:, t, :], scalar=1.0, in1=cand[:], op0=ALU.subtract, op1=ALU.mult
+                )
+                result = gate.tile([P, NODES], F32, name="result")
+                nc.vector.tensor_tensor(out=result[:], in0=u_hx[:, t, :], in1=minus[:], op=ALU.subtract)
+                nc.sync.dma_start(out=out[b, a * P : (a + 1) * P, :], in_=result[:])
+
+        block_order = (X2[0], X2[1], X0, X1[0], X1[1])
+        whole = (NODES,)
+        nodes_to_partitions(s_rows[0], s_mx[0])
+        nodes_to_partitions(x1_rows[0][0], x1_mx[0][0])
+        nodes_to_partitions(s_rows[1], s_mx[1])
+        nodes_to_partitions(x1_rows[1][0], x1_mx[1][0])
+        diffusion_step(0, 0)
+        nodes_to_partitions(x1_rows[0][1], x1_mx[0][1])
+        diffusion_step(1, 0)
+        nodes_to_partitions(x1_rows[1][1], x1_mx[1][1])
+        diffusion_step(0, 1)
+        diffusion_step(1, 1)
+        channels_side_by_side(x0_rows[0], NODES, h_mx[0][X0], whole)
+        for g in range(GRAPHS):
+            channels_side_by_side(x1_rows[g][0], NODES, h_mx[0][X1[g]], whole)
+        for i in range(BLOCKS):
+            channels_side_by_side(w_rows[i], HID, w_mx[i], (2 * P, P))
+        mix_channels(0, block_order)
+        channels_side_by_side(x0_rows[1], NODES, h_mx[1][X0], whole)
+        for g in range(GRAPHS):
+            channels_side_by_side(x1_rows[g][1], NODES, h_mx[1][X1[g]], whole)
+        mix_channels(1, block_order)

@@ -21,7 +21,8 @@ HID = 384
 HID_TILES = HID // P
 BLOCKS = 5
 X0, X1, X2 = 0, (1, 3), (2, 4)
-HALF = NODES // 2
+PSUM_BANKS = 8
+SIDE_BUFS = 8
 
 FLOPS = 2 * GRAPHS * BATCH * CH * NODES * NODES + 2 * BATCH * BLOCKS * CH * HID * NODES
 
@@ -33,12 +34,11 @@ def tile_dcgrucell_pc_kernel(
     with ExitStack() as ctx:
         const = ctx.enter_context(tc.tile_pool(name="const", bufs=1))
         raw = ctx.enter_context(tc.tile_pool(name="raw", bufs=1))
-        side = ctx.enter_context(tc.tile_pool(name="side", bufs=6))
+        side = ctx.enter_context(tc.tile_pool(name="side", bufs=SIDE_BUFS))
         mx = ctx.enter_context(tc.tile_pool(name="mx", bufs=1))
         gate = ctx.enter_context(tc.tile_pool(name="gate", bufs=3))
-        flip_psum = ctx.enter_context(tc.psum_pool(name="flip_psum", bufs=2))
-        step_psum = ctx.enter_context(tc.psum_pool(name="step_psum", bufs=3))
-        mix_psum = ctx.enter_context(tc.psum_pool(name="mix_psum", bufs=HID_TILES))
+        psum = ctx.enter_context(tc.psum_pool(name="psum", bufs=PSUM_BANKS))
+        ctx.enter_context(tc.manual_schedule())
 
         def load_channels(x, b, name):
             rows = raw.tile([P, PACK * NODES], BF16, name=name)
@@ -56,8 +56,8 @@ def tile_dcgrucell_pc_kernel(
         x0_rows = [None] * BATCH
         x1_rows = [[None] * BATCH for g in range(GRAPHS)]
         s_rows = [None] * GRAPHS
-        s_rows[0] = load_support(support0, "s_rows0")
         x1_rows[0][0] = load_channels(x1_0, 0, "x1_rows00")
+        s_rows[0] = load_support(support0, "s_rows0")
         x0_rows[0] = load_channels(x_cand, 0, "x0_rows0")
         s_rows[1] = load_support(support1, "s_rows1")
         x1_rows[1][0] = load_channels(x1_1, 0, "x1_rows10")
@@ -83,7 +83,7 @@ def tile_dcgrucell_pc_kernel(
         with nc.allow_non_contiguous_dma(reason="384 bias values, one to a partition and tile"):
             nc.scalar.dma_start(out=bias_bf[:], in_=b_c.rearrange("(a p) -> p a", p=P))
         bias = const.tile([P, HID_TILES], F32, name="bias")
-        nc.vector.tensor_copy(out=bias[:], in_=bias_bf[:])
+        nc.gpsimd.tensor_copy(out=bias[:], in_=bias_bf[:])
         warm = const.tile([P, 1], F32, name="warm")
         nc.scalar.activation(out=warm[:], in_=ident[:, 0:1], func=ACT.Tanh)
 
@@ -92,11 +92,16 @@ def tile_dcgrucell_pc_kernel(
             scales = mx.tile([P, width], U8, name=name + "_scales", align_bytes=64)
             return codes, scales
 
-        def quantise(operand, cols, values):
+        def quantise(packed, operand, widths):
             codes, scales = operand
-            nc.vector.quantize_mx(
-                out=codes[:, cols].bitcast(FP8X4), scales=scales[:, cols], in_=values
-            )
+            first = 0
+            for w in widths:
+                nc.vector.quantize_mx(
+                    out=codes[:, first : first + w].bitcast(FP8X4),
+                    scales=scales[:, first : first + w],
+                    in_=packed[:, first * PACK : (first + w) * PACK],
+                )
+                first += w
 
         def mx_pass(acc, stationary, s_cols, moving, m_cols, start, stop):
             nc.tensor.matmul_mx(
@@ -114,12 +119,12 @@ def tile_dcgrucell_pc_kernel(
         h_mx = [[mx_operand(NODES, "h_mx%d%d" % (b, i)) for i in range(BLOCKS)] for b in range(BATCH)]
         w_mx = [mx_operand(HID, "w_mx%d" % i) for i in range(BLOCKS)]
 
-        def nodes_to_partitions(rows, operand):
+        def nodes_to_partitions(rows):
             words = rows[:].bitcast(F32).rearrange("p (s w) -> p s w", s=PACK)
             packed = side.tile([P, PACK * CH], BF16, name="packed", tag="side", align_bytes=64)
             packed_words = packed[:].bitcast(F32).rearrange("p (c v) -> p c v", v=2)
             for pair in range(2):
-                bank = flip_psum.tile([P, 2, 2 * P], F32, name="flip_bank")
+                bank = psum.tile([P, 2, 2 * P], F32, name="flip_bank", tag="bank")
                 for s in range(2):
                     for v in range(2):
                         nc.tensor.transpose(
@@ -131,18 +136,15 @@ def tile_dcgrucell_pc_kernel(
                     out=packed_words[:, pair * 2 * P : (pair + 1) * 2 * P, :],
                     in_=bank[:].rearrange("p v c -> p c v"),
                 )
-            quantise(operand, slice(0, CH), packed[:])
+            return packed
 
-        def channels_side_by_side(rows, width, operand, widths):
+        def channels_side_by_side(copy, rows, width):
             packed = side.tile([P, width * PACK], BF16, name="packed", tag="side", align_bytes=64)
-            nc.scalar.copy(
+            copy(
                 out=packed[:].rearrange("p (c i j) -> p c j i", i=4, j=PACK),
                 in_=rows[:].rearrange("p (j c i) -> p c j i", j=PACK, i=4),
             )
-            first = 0
-            for w in widths:
-                quantise(operand, slice(first, first + w), packed[:, first * PACK : (first + w) * PACK])
-                first += w
+            return packed
 
         def diffusion_step(g, b):
             packed = side.tile([P, NODES * PACK], BF16, name="packed", tag="side", align_bytes=64)
@@ -150,7 +152,7 @@ def tile_dcgrucell_pc_kernel(
             x0_jn = x0_rows[b][:].rearrange("p (j n) -> p j n", j=PACK)
             for r in range(NODES // P):
                 nodes = slice(r * P, (r + 1) * P)
-                bank = step_psum.tile([P, PACK, P], F32, name="step_bank")
+                bank = psum.tile([P, PACK, P], F32, name="step_bank", tag="bank")
                 for j in range(PACK):
                     mx_pass(bank[:, j, :], x1_mx[g][b], slice(j * P, (j + 1) * P), s_mx[g], nodes, True, True)
                 nc.vector.scalar_tensor_tensor(
@@ -161,48 +163,95 @@ def tile_dcgrucell_pc_kernel(
                     op0=ALU.mult,
                     op1=ALU.subtract,
                 )
-            quantise(h_mx[b][X2[g]], slice(0, NODES), packed[:])
+            return packed
 
         u_hx = const.tile([P, BATCH * HID_TILES, NODES], F32, name="u_hx")
 
-        def mix_channels(b, block_order):
+        def gate_state(b):
             tiles = slice(b * HID_TILES, (b + 1) * HID_TILES)
-            nc.vector.tensor_tensor(out=u_hx[:, tiles, :], in0=u_rows[:, tiles, :], in1=hx_rows[:, tiles, :], op=ALU.mult)
-            accs = [mix_psum.tile([P, NODES], F32, name="mix_acc") for a in range(HID_TILES)]
+            nc.vector.tensor_tensor(
+                out=u_hx[:, tiles, :], in0=u_rows[:, tiles, :], in1=hx_rows[:, tiles, :], op=ALU.mult
+            )
+
+        def mix_channels(b, block_order):
+            accs = [psum.tile([P, NODES], F32, name="mix_acc", tag="bank") for a in range(HID_TILES)]
             for k, i in enumerate(block_order):
                 for a in range(HID_TILES):
-                    mx_pass(accs[a][:], w_mx[i], slice(a * P, (a + 1) * P), h_mx[b][i], slice(0, NODES), k == 0, k == BLOCKS - 1)
-            for a in range(HID_TILES):
-                t = b * HID_TILES + a
-                cand = gate.tile([P, NODES], F32, name="cand")
-                nc.scalar.activation(out=cand[:], in_=accs[a][:], func=ACT.Tanh, bias=bias[:, a : a + 1], scale=1.0)
-                minus = gate.tile([P, NODES], F32, name="minus")
-                nc.vector.scalar_tensor_tensor(
-                    out=minus[:], in0=u_rows[:, t, :], scalar=1.0, in1=cand[:], op0=ALU.subtract, op1=ALU.mult
-                )
-                result = gate.tile([P, NODES], F32, name="result")
-                nc.vector.tensor_tensor(out=result[:], in0=u_hx[:, t, :], in1=minus[:], op=ALU.subtract)
-                nc.sync.dma_start(out=out[b, a * P : (a + 1) * P, :], in_=result[:])
+                    mx_pass(
+                        accs[a][:], w_mx[i], slice(a * P, (a + 1) * P), h_mx[b][i], slice(0, NODES),
+                        k == 0, k == BLOCKS - 1,
+                    )
+            return accs
 
-        block_order = (X2[0], X2[1], X0, X1[0], X1[1])
+        def candidate(acc, a):
+            cand = gate.tile([P, NODES], F32, name="cand")
+            nc.scalar.activation(out=cand[:], in_=acc[:], func=ACT.Tanh, bias=bias[:, a : a + 1], scale=1.0)
+            return cand
+
+        def blend_and_store(b, a, cand):
+            t = b * HID_TILES + a
+            minus = gate.tile([P, NODES], F32, name="minus")
+            nc.vector.scalar_tensor_tensor(
+                out=minus[:], in0=u_rows[:, t, :], scalar=1.0, in1=cand[:], op0=ALU.subtract, op1=ALU.mult
+            )
+            result = gate.tile([P, NODES], F32, name="result")
+            nc.vector.tensor_tensor(out=result[:], in0=u_hx[:, t, :], in1=minus[:], op=ALU.subtract)
+            nc.sync.dma_start(out=out[b, a * P : (a + 1) * P, :], in_=result[:])
+
         whole = (NODES,)
-        nodes_to_partitions(s_rows[0], s_mx[0])
-        nodes_to_partitions(x1_rows[0][0], x1_mx[0][0])
-        nodes_to_partitions(s_rows[1], s_mx[1])
-        nodes_to_partitions(x1_rows[1][0], x1_mx[1][0])
-        diffusion_step(0, 0)
-        nodes_to_partitions(x1_rows[0][1], x1_mx[0][1])
-        diffusion_step(1, 0)
-        nodes_to_partitions(x1_rows[1][1], x1_mx[1][1])
-        diffusion_step(0, 1)
-        diffusion_step(1, 1)
-        channels_side_by_side(x0_rows[0], NODES, h_mx[0][X0], whole)
-        for g in range(GRAPHS):
-            channels_side_by_side(x1_rows[g][0], NODES, h_mx[0][X1[g]], whole)
-        for i in range(BLOCKS):
-            channels_side_by_side(w_rows[i], HID, w_mx[i], (2 * P, P))
-        mix_channels(0, block_order)
-        channels_side_by_side(x0_rows[1], NODES, h_mx[1][X0], whole)
-        for g in range(GRAPHS):
-            channels_side_by_side(x1_rows[g][1], NODES, h_mx[1][X1[g]], whole)
-        mix_channels(1, block_order)
+        w_widths = (2 * P, P)
+        on_scalar = nc.scalar.copy
+        on_vector = nc.vector.tensor_copy
+
+        flip_x1 = nodes_to_partitions(x1_rows[0][0])
+        near_x1 = channels_side_by_side(on_vector, x1_rows[0][0], NODES)
+        quantise(near_x1, h_mx[0][X1[0]], whole)
+        flip_s = nodes_to_partitions(s_rows[0])
+        quantise(flip_x1, x1_mx[0][0], whole)
+        quantise(flip_s, s_mx[0], whole)
+        x2 = diffusion_step(0, 0)
+        near_x0 = channels_side_by_side(on_scalar, x0_rows[0], NODES)
+        flip_s = nodes_to_partitions(s_rows[1])
+        flip_x1 = nodes_to_partitions(x1_rows[1][0])
+        quantise(near_x0, h_mx[0][X0], whole)
+        quantise(flip_s, s_mx[1], whole)
+        quantise(x2, h_mx[0][X2[0]], whole)
+        quantise(flip_x1, x1_mx[1][0], whole)
+        flip_x1_0 = nodes_to_partitions(x1_rows[0][1])
+        flip_x1_1 = nodes_to_partitions(x1_rows[1][1])
+        x2 = diffusion_step(1, 0)
+        quantise(flip_x1_0, x1_mx[0][1], whole)
+        quantise(x2, h_mx[0][X2[1]], whole)
+        quantise(flip_x1_1, x1_mx[1][1], whole)
+        near_x1 = channels_side_by_side(on_scalar, x1_rows[1][0], NODES)
+        near_w = [channels_side_by_side(on_scalar, w_rows[0], HID)]
+        x2 = diffusion_step(0, 1)
+        quantise(near_x1, h_mx[0][X1[1]], whole)
+        quantise(x2, h_mx[1][X2[0]], whole)
+        near_w.append(channels_side_by_side(on_scalar, w_rows[1], HID))
+        near_w.append(channels_side_by_side(on_scalar, w_rows[2], HID))
+        quantise(near_w[0], w_mx[0], w_widths)
+        x2 = diffusion_step(1, 1)
+        quantise(near_w[1], w_mx[1], w_widths)
+        quantise(x2, h_mx[1][X2[1]], whole)
+        quantise(near_w[2], w_mx[2], w_widths)
+        near_w.append(channels_side_by_side(on_scalar, w_rows[3], HID))
+        near_w.append(channels_side_by_side(on_scalar, w_rows[4], HID))
+        gate_state(0)
+        quantise(near_w[3], w_mx[3], w_widths)
+        quantise(near_w[4], w_mx[4], w_widths)
+        accs = mix_channels(0, (0, 1, 2, 3, 4))
+        near_x0 = channels_side_by_side(on_scalar, x0_rows[1], NODES)
+        gate_state(1)
+        quantise(near_x0, h_mx[1][X0], whole)
+        near_x1_0 = channels_side_by_side(on_scalar, x1_rows[0][1], NODES)
+        cands = [candidate(accs[a], a) for a in range(HID_TILES)]
+        near_x1_1 = channels_side_by_side(on_scalar, x1_rows[1][1], NODES)
+        quantise(near_x1_0, h_mx[1][X1[0]], whole)
+        blend_and_store(0, 0, cands[0])
+        blend_and_store(0, 1, cands[1])
+        quantise(near_x1_1, h_mx[1][X1[1]], whole)
+        blend_and_store(0, 2, cands[2])
+        accs = mix_channels(1, (X2[0], X2[1], X0, X1[0], X1[1]))
+        for a in range(HID_TILES):
+            blend_and_store(1, a, candidate(accs[a], a))

@@ -64,6 +64,10 @@ def tile_dcgrucell_pc_kernel(
         x1_rows[0][1] = load_channels(x1_0, 1, "x1_rows01")
         x1_rows[1][1] = load_channels(x1_1, 1, "x1_rows11")
         x0_rows[1] = load_channels(x_cand, 1, "x0_rows1")
+        hx_rows = raw.tile([P, BATCH * HID_TILES, NODES], BF16, name="hx_rows")
+        nc.sync.dma_start(out=hx_rows[:], in_=hx.rearrange("b (a p) n -> p (b a) n", p=P))
+        u_rows = raw.tile([P, BATCH * HID_TILES, NODES], BF16, name="u_rows")
+        nc.sync.dma_start(out=u_rows[:], in_=u.rearrange("b (a p) n -> p (b a) n", p=P))
         w_rows = []
         for i in range(BLOCKS):
             rows = raw.tile([P, PACK * HID], BF16, name="w_rows%d" % i)
@@ -72,10 +76,6 @@ def tile_dcgrucell_pc_kernel(
                 in_=W_c[i * CH : (i + 1) * CH, :].rearrange("(p j) o -> p (j o)", j=PACK),
             )
             w_rows.append(rows)
-        hx_rows = raw.tile([P, BATCH * HID_TILES, NODES], BF16, name="hx_rows")
-        nc.sync.dma_start(out=hx_rows[:], in_=hx.rearrange("b (a p) n -> p (b a) n", p=P))
-        u_rows = raw.tile([P, BATCH * HID_TILES, NODES], BF16, name="u_rows")
-        nc.sync.dma_start(out=u_rows[:], in_=u.rearrange("b (a p) n -> p (b a) n", p=P))
 
         ident = const.tile([P, P], F32, name="ident")
         make_identity(nc, ident[:])
@@ -167,21 +167,12 @@ def tile_dcgrucell_pc_kernel(
 
         u_hx = const.tile([P, BATCH * HID_TILES, NODES], F32, name="u_hx")
 
-        def gate_state(b):
-            tiles = slice(b * HID_TILES, (b + 1) * HID_TILES)
-            nc.vector.tensor_tensor(
-                out=u_hx[:, tiles, :], in0=u_rows[:, tiles, :], in1=hx_rows[:, tiles, :], op=ALU.mult
-            )
+        def gate_state(t):
+            nc.gpsimd.tensor_tensor(out=u_hx[:, t, :], in0=u_rows[:, t, :], in1=hx_rows[:, t, :], op=ALU.mult)
 
-        def mix_channels(b, block_order):
-            accs = [psum.tile([P, NODES], F32, name="mix_acc", tag="bank") for a in range(HID_TILES)]
-            for k, i in enumerate(block_order):
-                for a in range(HID_TILES):
-                    mx_pass(
-                        accs[a][:], w_mx[i], slice(a * P, (a + 1) * P), h_mx[b][i], slice(0, NODES),
-                        k == 0, k == BLOCKS - 1,
-                    )
-            return accs
+        def mix_block(accs, b, i, first, last):
+            for a in range(HID_TILES):
+                mx_pass(accs[a][:], w_mx[i], slice(a * P, (a + 1) * P), h_mx[b][i], slice(0, NODES), first, last)
 
         def candidate(acc, a):
             cand = gate.tile([P, NODES], F32, name="cand")
@@ -206,52 +197,59 @@ def tile_dcgrucell_pc_kernel(
         flip_x1 = nodes_to_partitions(x1_rows[0][0])
         near_x1 = channels_side_by_side(on_vector, x1_rows[0][0], NODES)
         quantise(near_x1, h_mx[0][X1[0]], whole)
-        flip_s = nodes_to_partitions(s_rows[0])
+        flip_s0 = nodes_to_partitions(s_rows[0])
         quantise(flip_x1, x1_mx[0][0], whole)
-        quantise(flip_s, s_mx[0], whole)
+        flip_s1 = nodes_to_partitions(s_rows[1])
+        quantise(flip_s0, s_mx[0], whole)
+        near_x0 = channels_side_by_side(on_vector, x0_rows[0], NODES)
         x2 = diffusion_step(0, 0)
-        near_x0 = channels_side_by_side(on_scalar, x0_rows[0], NODES)
-        flip_s = nodes_to_partitions(s_rows[1])
         flip_x1 = nodes_to_partitions(x1_rows[1][0])
-        quantise(near_x0, h_mx[0][X0], whole)
-        quantise(flip_s, s_mx[1], whole)
-        quantise(x2, h_mx[0][X2[0]], whole)
-        quantise(flip_x1, x1_mx[1][0], whole)
         flip_x1_0 = nodes_to_partitions(x1_rows[0][1])
         flip_x1_1 = nodes_to_partitions(x1_rows[1][1])
+        quantise(flip_s1, s_mx[1], whole)
+        quantise(flip_x1, x1_mx[1][0], whole)
+        quantise(near_x0, h_mx[0][X0], whole)
+        quantise(x2, h_mx[0][X2[0]], whole)
         x2 = diffusion_step(1, 0)
-        quantise(flip_x1_0, x1_mx[0][1], whole)
-        quantise(x2, h_mx[0][X2[1]], whole)
-        quantise(flip_x1_1, x1_mx[1][1], whole)
         near_x1 = channels_side_by_side(on_scalar, x1_rows[1][0], NODES)
+        quantise(flip_x1_0, x1_mx[0][1], whole)
+        quantise(flip_x1_1, x1_mx[1][1], whole)
+        quantise(x2, h_mx[0][X2[1]], whole)
         near_w = [channels_side_by_side(on_scalar, w_rows[0], HID)]
-        x2 = diffusion_step(0, 1)
         quantise(near_x1, h_mx[0][X1[1]], whole)
-        quantise(x2, h_mx[1][X2[0]], whole)
-        near_w.append(channels_side_by_side(on_scalar, w_rows[1], HID))
-        near_w.append(channels_side_by_side(on_scalar, w_rows[2], HID))
+        for t in range(BATCH * HID_TILES):
+            gate_state(t)
+        x2_0 = diffusion_step(0, 1)
+        x2_1 = diffusion_step(1, 1)
+        for i in (1, 2, 3):
+            near_w.append(channels_side_by_side(on_scalar, w_rows[i], HID))
         quantise(near_w[0], w_mx[0], w_widths)
-        x2 = diffusion_step(1, 1)
+        quantise(x2_0, h_mx[1][X2[0]], whole)
         quantise(near_w[1], w_mx[1], w_widths)
-        quantise(x2, h_mx[1][X2[1]], whole)
+        quantise(x2_1, h_mx[1][X2[1]], whole)
         quantise(near_w[2], w_mx[2], w_widths)
-        near_w.append(channels_side_by_side(on_scalar, w_rows[3], HID))
         near_w.append(channels_side_by_side(on_scalar, w_rows[4], HID))
-        gate_state(0)
         quantise(near_w[3], w_mx[3], w_widths)
+        near_x1_1 = channels_side_by_side(on_vector, x1_rows[1][1], NODES)
         quantise(near_w[4], w_mx[4], w_widths)
-        accs = mix_channels(0, (0, 1, 2, 3, 4))
+        accs = [
+            [psum.tile([P, NODES], F32, name="mix_acc", tag="bank") for a in range(HID_TILES)]
+            for b in range(BATCH)
+        ]
+        for i in range(BLOCKS):
+            mix_block(accs[0], 0, i, i == 0, i == BLOCKS - 1)
+            if i in X2:
+                mix_block(accs[1], 1, i, i == X2[0], False)
         near_x0 = channels_side_by_side(on_scalar, x0_rows[1], NODES)
-        gate_state(1)
-        quantise(near_x0, h_mx[1][X0], whole)
         near_x1_0 = channels_side_by_side(on_scalar, x1_rows[0][1], NODES)
-        cands = [candidate(accs[a], a) for a in range(HID_TILES)]
-        near_x1_1 = channels_side_by_side(on_scalar, x1_rows[1][1], NODES)
-        quantise(near_x1_0, h_mx[1][X1[0]], whole)
-        blend_and_store(0, 0, cands[0])
-        blend_and_store(0, 1, cands[1])
         quantise(near_x1_1, h_mx[1][X1[1]], whole)
-        blend_and_store(0, 2, cands[2])
-        accs = mix_channels(1, (X2[0], X2[1], X0, X1[0], X1[1]))
+        quantise(near_x0, h_mx[1][X0], whole)
+        cands = [candidate(accs[0][a], a) for a in range(HID_TILES)]
+        quantise(near_x1_0, h_mx[1][X1[0]], whole)
         for a in range(HID_TILES):
-            blend_and_store(1, a, candidate(accs[a], a))
+            blend_and_store(0, a, cands[a])
+        mix_block(accs[1], 1, X1[1], False, False)
+        mix_block(accs[1], 1, X0, False, False)
+        mix_block(accs[1], 1, X1[0], False, True)
+        for a in range(HID_TILES):
+            blend_and_store(1, a, candidate(accs[1][a], a))

@@ -21,8 +21,9 @@ HID = 384
 HID_TILES = HID // P
 BLOCKS = 5
 X0, X1, X2 = 0, (1, 3), (2, 4)
+MIX_ORDER = (X2[0], X2[1], X1[1], X0, X1[0])
 PSUM_BANKS = 8
-SIDE_BUFS = 8
+SIDE_BUFS = 10
 
 FLOPS = 2 * GRAPHS * BATCH * CH * NODES * NODES + 2 * BATCH * BLOCKS * CH * HID * NODES
 
@@ -35,47 +36,50 @@ def tile_dcgrucell_pc_kernel(
         const = ctx.enter_context(tc.tile_pool(name="const", bufs=1))
         raw = ctx.enter_context(tc.tile_pool(name="raw", bufs=1))
         side = ctx.enter_context(tc.tile_pool(name="side", bufs=SIDE_BUFS))
+        w_side = ctx.enter_context(tc.tile_pool(name="w_side", bufs=BLOCKS))
         mx = ctx.enter_context(tc.tile_pool(name="mx", bufs=1))
-        gate = ctx.enter_context(tc.tile_pool(name="gate", bufs=3))
+        gate = ctx.enter_context(tc.tile_pool(name="gate", bufs=BATCH * HID_TILES))
         psum = ctx.enter_context(tc.psum_pool(name="psum", bufs=PSUM_BANKS))
         ctx.enter_context(tc.manual_schedule())
 
-        def load_channels(x, b, name):
+        def load_row_sets(view, name, pieces):
             rows = raw.tile([P, PACK * NODES], BF16, name=name)
-            nc.sync.dma_start(out=rows[:], in_=x[b].rearrange("(p j) n -> p (j n)", j=PACK))
+            rows_sn = rows[:].rearrange("p (s n) -> p s n", s=PACK)
+            sets = PACK // pieces
+            for k in range(pieces):
+                nc.sync.dma_start(
+                    out=rows_sn[:, k * sets : (k + 1) * sets, :], in_=view[:, k * sets : (k + 1) * sets, :]
+                )
             return rows
 
+        def load_channels(x, b, name, pieces):
+            return load_row_sets(x[b].rearrange("(p j) n -> p j n", j=PACK), name, pieces)
+
         def load_support(support, name):
-            rows = raw.tile([P, PACK * NODES], BF16, name=name)
-            nc.sync.dma_start(
-                out=rows[:].rearrange("p (a n) -> p a n", a=PACK),
-                in_=support.rearrange("(a p) n -> p a n", p=P),
-            )
-            return rows
+            return load_row_sets(support.rearrange("(a p) n -> p a n", p=P), name, 2)
 
         x0_rows = [None] * BATCH
         x1_rows = [[None] * BATCH for g in range(GRAPHS)]
         s_rows = [None] * GRAPHS
-        x1_rows[0][0] = load_channels(x1_0, 0, "x1_rows00")
+        x1_rows[0][0] = load_channels(x1_0, 0, "x1_rows00", 2)
         s_rows[0] = load_support(support0, "s_rows0")
-        x0_rows[0] = load_channels(x_cand, 0, "x0_rows0")
+        x0_rows[0] = load_channels(x_cand, 0, "x0_rows0", 1)
         s_rows[1] = load_support(support1, "s_rows1")
-        x1_rows[1][0] = load_channels(x1_1, 0, "x1_rows10")
-        x1_rows[0][1] = load_channels(x1_0, 1, "x1_rows01")
-        x1_rows[1][1] = load_channels(x1_1, 1, "x1_rows11")
-        x0_rows[1] = load_channels(x_cand, 1, "x0_rows1")
+        x1_rows[1][0] = load_channels(x1_1, 0, "x1_rows10", 2)
+        x1_rows[0][1] = load_channels(x1_0, 1, "x1_rows01", 2)
+        x1_rows[1][1] = load_channels(x1_1, 1, "x1_rows11", 2)
+        x0_rows[1] = load_channels(x_cand, 1, "x0_rows1", 1)
         hx_rows = raw.tile([P, BATCH * HID_TILES, NODES], BF16, name="hx_rows")
         nc.sync.dma_start(out=hx_rows[:], in_=hx.rearrange("b (a p) n -> p (b a) n", p=P))
         u_rows = raw.tile([P, BATCH * HID_TILES, NODES], BF16, name="u_rows")
         nc.sync.dma_start(out=u_rows[:], in_=u.rearrange("b (a p) n -> p (b a) n", p=P))
-        w_rows = []
-        for i in range(BLOCKS):
-            rows = raw.tile([P, PACK * HID], BF16, name="w_rows%d" % i)
+        w_rows = [None] * BLOCKS
+        for i in MIX_ORDER:
+            w_rows[i] = raw.tile([P, PACK * HID], BF16, name="w_rows%d" % i)
             nc.sync.dma_start(
-                out=rows[:],
+                out=w_rows[i][:],
                 in_=W_c[i * CH : (i + 1) * CH, :].rearrange("(p j) o -> p (j o)", j=PACK),
             )
-            w_rows.append(rows)
 
         ident = const.tile([P, P], F32, name="ident")
         make_identity(nc, ident[:])
@@ -138,12 +142,13 @@ def tile_dcgrucell_pc_kernel(
                 )
             return packed
 
-        def channels_side_by_side(copy, rows, width):
-            packed = side.tile([P, width * PACK], BF16, name="packed", tag="side", align_bytes=64)
-            copy(
-                out=packed[:].rearrange("p (c i j) -> p c j i", i=4, j=PACK),
-                in_=rows[:].rearrange("p (j c i) -> p c j i", j=PACK, i=4),
-            )
+        def channels_side_by_side(copy, rows, width, pieces=1, pool=side):
+            packed = pool.tile([P, width * PACK], BF16, name="packed", tag="side", align_bytes=64)
+            to = packed[:].rearrange("p (c i j) -> p c j i", i=4, j=PACK)
+            frm = rows[:].rearrange("p (j c i) -> p c j i", j=PACK, i=4)
+            runs = width // 4 // pieces
+            for k in range(pieces):
+                copy(out=to[:, k * runs : (k + 1) * runs], in_=frm[:, k * runs : (k + 1) * runs])
             return packed
 
         def diffusion_step(g, b):
@@ -166,6 +171,7 @@ def tile_dcgrucell_pc_kernel(
             return packed
 
         u_hx = const.tile([P, BATCH * HID_TILES, NODES], F32, name="u_hx")
+        out_tiles = out.rearrange("b (a p) n -> (b a) p n", p=P)
 
         def gate_state(t):
             nc.gpsimd.tensor_tensor(out=u_hx[:, t, :], in0=u_rows[:, t, :], in1=hx_rows[:, t, :], op=ALU.mult)
@@ -179,15 +185,17 @@ def tile_dcgrucell_pc_kernel(
             nc.scalar.activation(out=cand[:], in_=acc[:], func=ACT.Tanh, bias=bias[:, a : a + 1], scale=1.0)
             return cand
 
-        def blend_and_store(b, a, cand):
-            t = b * HID_TILES + a
+        def gate_candidate(t, cand):
             minus = gate.tile([P, NODES], F32, name="minus")
             nc.vector.scalar_tensor_tensor(
                 out=minus[:], in0=u_rows[:, t, :], scalar=1.0, in1=cand[:], op0=ALU.subtract, op1=ALU.mult
             )
+            return minus
+
+        def blend_and_store(t, minus):
             result = gate.tile([P, NODES], F32, name="result")
             nc.vector.tensor_tensor(out=result[:], in0=u_hx[:, t, :], in1=minus[:], op=ALU.subtract)
-            nc.sync.dma_start(out=out[b, a * P : (a + 1) * P, :], in_=result[:])
+            nc.sync.dma_start(out=out_tiles[t], in_=result[:])
 
         whole = (NODES,)
         w_widths = (2 * P, P)
@@ -195,13 +203,13 @@ def tile_dcgrucell_pc_kernel(
         on_vector = nc.vector.tensor_copy
 
         flip_x1 = nodes_to_partitions(x1_rows[0][0])
-        near_x1 = channels_side_by_side(on_vector, x1_rows[0][0], NODES)
+        near_x1 = channels_side_by_side(on_vector, x1_rows[0][0], NODES, 2)
         quantise(near_x1, h_mx[0][X1[0]], whole)
         flip_s0 = nodes_to_partitions(s_rows[0])
         quantise(flip_x1, x1_mx[0][0], whole)
         flip_s1 = nodes_to_partitions(s_rows[1])
         quantise(flip_s0, s_mx[0], whole)
-        near_x0 = channels_side_by_side(on_vector, x0_rows[0], NODES)
+        near_x0 = channels_side_by_side(on_vector, x0_rows[0], NODES, 2)
         x2 = diffusion_step(0, 0)
         flip_x1 = nodes_to_partitions(x1_rows[1][0])
         flip_x1_0 = nodes_to_partitions(x1_rows[0][1])
@@ -210,46 +218,45 @@ def tile_dcgrucell_pc_kernel(
         quantise(flip_x1, x1_mx[1][0], whole)
         quantise(near_x0, h_mx[0][X0], whole)
         quantise(x2, h_mx[0][X2[0]], whole)
-        x2 = diffusion_step(1, 0)
-        near_x1 = channels_side_by_side(on_scalar, x1_rows[1][0], NODES)
         quantise(flip_x1_0, x1_mx[0][1], whole)
         quantise(flip_x1_1, x1_mx[1][1], whole)
-        quantise(x2, h_mx[0][X2[1]], whole)
-        near_w = [channels_side_by_side(on_scalar, w_rows[0], HID)]
-        quantise(near_x1, h_mx[0][X1[1]], whole)
         for t in range(BATCH * HID_TILES):
             gate_state(t)
-        x2_0 = diffusion_step(0, 1)
-        x2_1 = diffusion_step(1, 1)
-        for i in (1, 2, 3):
-            near_w.append(channels_side_by_side(on_scalar, w_rows[i], HID))
-        quantise(near_w[0], w_mx[0], w_widths)
-        quantise(x2_0, h_mx[1][X2[0]], whole)
-        quantise(near_w[1], w_mx[1], w_widths)
-        quantise(x2_1, h_mx[1][X2[1]], whole)
-        quantise(near_w[2], w_mx[2], w_widths)
-        near_w.append(channels_side_by_side(on_scalar, w_rows[4], HID))
-        quantise(near_w[3], w_mx[3], w_widths)
+        near_x1 = channels_side_by_side(on_scalar, x1_rows[1][0], NODES)
+        near_w = [None] * BLOCKS
+        for i in MIX_ORDER:
+            near_w[i] = channels_side_by_side(on_scalar, w_rows[i], HID, pool=w_side)
+        x2_10 = diffusion_step(1, 0)
+        x2_01 = diffusion_step(0, 1)
+        x2_11 = diffusion_step(1, 1)
+        quantise(x2_10, h_mx[0][X2[1]], whole)
+        quantise(near_w[X2[0]], w_mx[X2[0]], w_widths)
+        quantise(x2_01, h_mx[1][X2[0]], whole)
+        quantise(near_w[X2[1]], w_mx[X2[1]], w_widths)
+        quantise(x2_11, h_mx[1][X2[1]], whole)
+        quantise(near_x1, h_mx[0][X1[1]], whole)
+        quantise(near_w[X1[1]], w_mx[X1[1]], w_widths)
+        quantise(near_w[X0], w_mx[X0], w_widths)
         near_x1_1 = channels_side_by_side(on_vector, x1_rows[1][1], NODES)
-        quantise(near_w[4], w_mx[4], w_widths)
+        quantise(near_w[X1[0]], w_mx[X1[0]], w_widths)
         accs = [
             [psum.tile([P, NODES], F32, name="mix_acc", tag="bank") for a in range(HID_TILES)]
             for b in range(BATCH)
         ]
-        for i in range(BLOCKS):
-            mix_block(accs[0], 0, i, i == 0, i == BLOCKS - 1)
+        for i in MIX_ORDER:
+            mix_block(accs[0], 0, i, i == MIX_ORDER[0], i == MIX_ORDER[-1])
             if i in X2:
-                mix_block(accs[1], 1, i, i == X2[0], False)
+                mix_block(accs[1], 1, i, i == MIX_ORDER[0], False)
         near_x0 = channels_side_by_side(on_scalar, x0_rows[1], NODES)
         near_x1_0 = channels_side_by_side(on_scalar, x1_rows[0][1], NODES)
         quantise(near_x1_1, h_mx[1][X1[1]], whole)
         quantise(near_x0, h_mx[1][X0], whole)
-        cands = [candidate(accs[0][a], a) for a in range(HID_TILES)]
         quantise(near_x1_0, h_mx[1][X1[0]], whole)
-        for a in range(HID_TILES):
-            blend_and_store(0, a, cands[a])
-        mix_block(accs[1], 1, X1[1], False, False)
-        mix_block(accs[1], 1, X0, False, False)
-        mix_block(accs[1], 1, X1[0], False, True)
-        for a in range(HID_TILES):
-            blend_and_store(1, a, candidate(accs[1][a], a))
+        for i in MIX_ORDER[GRAPHS:]:
+            mix_block(accs[1], 1, i, False, i == MIX_ORDER[-1])
+        cands = [candidate(accs[b][a], a) for b in range(BATCH) for a in range(HID_TILES)]
+        minus = [gate_candidate(0, cands[0])]
+        for t in range(1, BATCH * HID_TILES):
+            minus.append(gate_candidate(t, cands[t]))
+            blend_and_store(t - 1, minus[t - 1])
+        blend_and_store(BATCH * HID_TILES - 1, minus[-1])

@@ -23,7 +23,7 @@ BLOCKS = 5
 X0, X1, X2 = 0, (1, 3), (2, 4)
 MIX_ORDER = (X2[0], X2[1], X1[1], X0, X1[0])
 PSUM_BANKS = 8
-SIDE_BUFS = 10
+SIDE_BUFS = 14
 
 FLOPS = 2 * GRAPHS * BATCH * CH * NODES * NODES + 2 * BATCH * BLOCKS * CH * HID * NODES
 
@@ -55,14 +55,14 @@ def tile_dcgrucell_pc_kernel(
         def load_channels(x, b, name, pieces):
             return load_row_sets(x[b].rearrange("(p j) n -> p j n", j=PACK), name, pieces)
 
-        def load_support(support, name):
-            return load_row_sets(support.rearrange("(a p) n -> p a n", p=P), name, 2)
+        def load_support(support, name, pieces=2):
+            return load_row_sets(support.rearrange("(a p) n -> p a n", p=P), name, pieces)
 
         x0_rows = [None] * BATCH
         x1_rows = [[None] * BATCH for g in range(GRAPHS)]
         s_rows = [None] * GRAPHS
-        x1_rows[0][0] = load_channels(x1_0, 0, "x1_rows00", 2)
-        s_rows[0] = load_support(support0, "s_rows0")
+        x1_rows[0][0] = load_channels(x1_0, 0, "x1_rows00", 4)
+        s_rows[0] = load_support(support0, "s_rows0", 4)
         x0_rows[0] = load_channels(x_cand, 0, "x0_rows0", 1)
         s_rows[1] = load_support(support1, "s_rows1")
         x1_rows[1][0] = load_channels(x1_1, 0, "x1_rows10", 2)
@@ -83,6 +83,8 @@ def tile_dcgrucell_pc_kernel(
 
         ident = const.tile([P, P], F32, name="ident")
         make_identity(nc, ident[:])
+        ident_bf = const.tile([P, P], BF16, name="ident_bf")
+        make_identity(nc, ident_bf[:])
         bias_bf = const.tile([P, HID_TILES], BF16, name="bias_bf")
         with nc.allow_non_contiguous_dma(reason="384 bias values, one to a partition and tile"):
             nc.scalar.dma_start(out=bias_bf[:], in_=b_c.rearrange("(a p) -> p a", p=P))
@@ -142,14 +144,24 @@ def tile_dcgrucell_pc_kernel(
                 )
             return packed
 
-        def channels_side_by_side(copy, rows, width, pieces=1, pool=side):
+        def side_tile(width=NODES, pool=side):
             packed = pool.tile([P, width * PACK], BF16, name="packed", tag="side", align_bytes=64)
+            return packed
+
+        def channels_side_by_side(copy, rows, packed, first, end):
             to = packed[:].rearrange("p (c i j) -> p c j i", i=4, j=PACK)
             frm = rows[:].rearrange("p (j c i) -> p c j i", j=PACK, i=4)
-            runs = width // 4 // pieces
-            for k in range(pieces):
-                copy(out=to[:, k * runs : (k + 1) * runs], in_=frm[:, k * runs : (k + 1) * runs])
-            return packed
+            copy(out=to[:, first // 4 : end // 4], in_=frm[:, first // 4 : end // 4])
+
+        def channels_through_tensor(rows, packed, half):
+            nodes = NODES // 2
+            bank = psum.tile([P, nodes * PACK], BF16, name="side_bank", tag="bank")
+            to = bank[:].rearrange("p (n j) -> p n j", j=PACK)
+            frm = rows[:].rearrange("p (j n) -> p n j", j=PACK)[:, half * nodes : (half + 1) * nodes, :]
+            for k in range(2):
+                part = slice(k * nodes // 2, (k + 1) * nodes // 2)
+                nc.tensor.matmul(out=to[:, part, :], lhsT=ident_bf[:], rhs=frm[:, part, :], start=True, stop=True)
+            nc.scalar.copy(out=packed[:, half * nodes * PACK : (half + 1) * nodes * PACK], in_=bank[:])
 
         def diffusion_step(g, b):
             packed = side.tile([P, NODES * PACK], BF16, name="packed", tag="side", align_bytes=64)
@@ -198,37 +210,60 @@ def tile_dcgrucell_pc_kernel(
             nc.sync.dma_start(out=out_tiles[t], in_=result[:])
 
         whole = (NODES,)
+        halves = (NODES // 2, NODES // 2)
         w_widths = (2 * P, P)
         on_scalar = nc.scalar.copy
         on_vector = nc.vector.tensor_copy
 
         flip_x1 = nodes_to_partitions(x1_rows[0][0])
-        near_x1 = channels_side_by_side(on_vector, x1_rows[0][0], NODES, 2)
+        near_x1 = side_tile()
+        channels_side_by_side(on_vector, x1_rows[0][0], near_x1, 0, NODES // 2)
+        channels_side_by_side(on_vector, x1_rows[0][0], near_x1, NODES // 2, NODES)
         quantise(near_x1, h_mx[0][X1[0]], whole)
         flip_s0 = nodes_to_partitions(s_rows[0])
         quantise(flip_x1, x1_mx[0][0], whole)
-        flip_s1 = nodes_to_partitions(s_rows[1])
-        quantise(flip_s0, s_mx[0], whole)
-        near_x0 = channels_side_by_side(on_vector, x0_rows[0], NODES, 2)
+        quantise(flip_s0, s_mx[0], halves)
+        near_x0_0 = side_tile()
+        channels_side_by_side(on_scalar, x0_rows[0], near_x0_0, 0, NODES // 2)
         x2 = diffusion_step(0, 0)
+        flip_s1 = nodes_to_partitions(s_rows[1])
         flip_x1 = nodes_to_partitions(x1_rows[1][0])
         flip_x1_0 = nodes_to_partitions(x1_rows[0][1])
         flip_x1_1 = nodes_to_partitions(x1_rows[1][1])
         quantise(flip_s1, s_mx[1], whole)
-        quantise(flip_x1, x1_mx[1][0], whole)
-        quantise(near_x0, h_mx[0][X0], whole)
         quantise(x2, h_mx[0][X2[0]], whole)
+        quantise(flip_x1, x1_mx[1][0], whole)
         quantise(flip_x1_0, x1_mx[0][1], whole)
         quantise(flip_x1_1, x1_mx[1][1], whole)
         for t in range(BATCH * HID_TILES):
             gate_state(t)
-        near_x1 = channels_side_by_side(on_scalar, x1_rows[1][0], NODES)
+        channels_side_by_side(on_scalar, x0_rows[0], near_x0_0, NODES // 2, NODES)
+        near_x1_1 = side_tile()
+        near_x0 = side_tile()
+        near_x1_0 = side_tile()
+        near_x1 = side_tile()
+        for half in range(2):
+            channels_through_tensor(x1_rows[1][0], near_x1, half)
         near_w = [None] * BLOCKS
-        for i in MIX_ORDER:
-            near_w[i] = channels_side_by_side(on_scalar, w_rows[i], HID, pool=w_side)
+
+        def regroup_w(i):
+            near_w[i] = side_tile(HID, w_side)
+            channels_side_by_side(on_scalar, w_rows[i], near_w[i], 0, HID)
+
         x2_10 = diffusion_step(1, 0)
+        channels_through_tensor(x1_rows[1][1], near_x1_1, 0)
+        regroup_w(MIX_ORDER[0])
         x2_01 = diffusion_step(0, 1)
+        channels_through_tensor(x1_rows[1][1], near_x1_1, 1)
+        regroup_w(MIX_ORDER[1])
         x2_11 = diffusion_step(1, 1)
+        for half in range(2):
+            channels_through_tensor(x0_rows[1], near_x0, half)
+        regroup_w(MIX_ORDER[2])
+        regroup_w(MIX_ORDER[3])
+        for half in range(2):
+            channels_through_tensor(x1_rows[0][1], near_x1_0, half)
+        regroup_w(MIX_ORDER[4])
         quantise(x2_10, h_mx[0][X2[1]], whole)
         quantise(near_w[X2[0]], w_mx[X2[0]], w_widths)
         quantise(x2_01, h_mx[1][X2[0]], whole)
@@ -236,8 +271,9 @@ def tile_dcgrucell_pc_kernel(
         quantise(x2_11, h_mx[1][X2[1]], whole)
         quantise(near_x1, h_mx[0][X1[1]], whole)
         quantise(near_w[X1[1]], w_mx[X1[1]], w_widths)
+        quantise(near_x0_0, h_mx[0][X0], whole)
         quantise(near_w[X0], w_mx[X0], w_widths)
-        near_x1_1 = channels_side_by_side(on_vector, x1_rows[1][1], NODES)
+        quantise(near_x1_1, h_mx[1][X1[1]], whole)
         quantise(near_w[X1[0]], w_mx[X1[0]], w_widths)
         accs = [
             [psum.tile([P, NODES], F32, name="mix_acc", tag="bank") for a in range(HID_TILES)]
@@ -247,9 +283,6 @@ def tile_dcgrucell_pc_kernel(
             mix_block(accs[0], 0, i, i == MIX_ORDER[0], i == MIX_ORDER[-1])
             if i in X2:
                 mix_block(accs[1], 1, i, i == MIX_ORDER[0], False)
-        near_x0 = channels_side_by_side(on_scalar, x0_rows[1], NODES)
-        near_x1_0 = channels_side_by_side(on_scalar, x1_rows[0][1], NODES)
-        quantise(near_x1_1, h_mx[1][X1[1]], whole)
         quantise(near_x0, h_mx[1][X0], whole)
         quantise(near_x1_0, h_mx[1][X1[0]], whole)
         for i in MIX_ORDER[GRAPHS:]:

@@ -22,6 +22,7 @@ HID_TILES = HID // P
 BLOCKS = 5
 X0, X1, X2 = 0, (1, 3), (2, 4)
 MIX_ORDER = (X2[0], X2[1], X1[1], X0, X1[0])
+EARLY_GATES = 5
 PSUM_BANKS = 8
 SIDE_BUFS = 14
 
@@ -61,18 +62,26 @@ def tile_dcgrucell_pc_kernel(
         x0_rows = [None] * BATCH
         x1_rows = [[None] * BATCH for g in range(GRAPHS)]
         s_rows = [None] * GRAPHS
-        x1_rows[0][0] = load_channels(x1_0, 0, "x1_rows00", 4)
-        s_rows[0] = load_support(support0, "s_rows0", 4)
+        x1_rows[0][0] = load_channels(x1_0, 0, "x1_rows00", 2)
+        s_rows[0] = load_support(support0, "s_rows0", 2)
         x0_rows[0] = load_channels(x_cand, 0, "x0_rows0", 1)
         s_rows[1] = load_support(support1, "s_rows1")
         x1_rows[1][0] = load_channels(x1_1, 0, "x1_rows10", 2)
         x1_rows[0][1] = load_channels(x1_0, 1, "x1_rows01", 2)
         x1_rows[1][1] = load_channels(x1_1, 1, "x1_rows11", 2)
-        x0_rows[1] = load_channels(x_cand, 1, "x0_rows1", 1)
         hx_rows = raw.tile([P, BATCH * HID_TILES, NODES], BF16, name="hx_rows")
-        nc.sync.dma_start(out=hx_rows[:], in_=hx.rearrange("b (a p) n -> p (b a) n", p=P))
         u_rows = raw.tile([P, BATCH * HID_TILES, NODES], BF16, name="u_rows")
-        nc.sync.dma_start(out=u_rows[:], in_=u.rearrange("b (a p) n -> p (b a) n", p=P))
+
+        hx_tiles = hx.rearrange("b (a p) n -> p (b a) n", p=P)
+        u_tiles = u.rearrange("b (a p) n -> p (b a) n", p=P)
+
+        def load_gate(first, end):
+            nc.sync.dma_start(out=hx_rows[:, first:end, :], in_=hx_tiles[:, first:end, :])
+            nc.sync.dma_start(out=u_rows[:, first:end, :], in_=u_tiles[:, first:end, :])
+
+        load_gate(0, EARLY_GATES - 1)
+        x0_rows[1] = load_channels(x_cand, 1, "x0_rows1", 1)
+        load_gate(EARLY_GATES - 1, EARLY_GATES)
         w_rows = [None] * BLOCKS
         for i in MIX_ORDER:
             w_rows[i] = raw.tile([P, PACK * HID], BF16, name="w_rows%d" % i)
@@ -80,6 +89,7 @@ def tile_dcgrucell_pc_kernel(
                 out=w_rows[i][:],
                 in_=W_c[i * CH : (i + 1) * CH, :].rearrange("(p j) o -> p (j o)", j=PACK),
             )
+        load_gate(EARLY_GATES, BATCH * HID_TILES)
 
         ident = const.tile([P, P], F32, name="ident")
         make_identity(nc, ident[:])
@@ -185,12 +195,11 @@ def tile_dcgrucell_pc_kernel(
         u_hx = const.tile([P, BATCH * HID_TILES, NODES], F32, name="u_hx")
         out_tiles = out.rearrange("b (a p) n -> (b a) p n", p=P)
 
-        def gate_state(t):
-            nc.gpsimd.tensor_tensor(out=u_hx[:, t, :], in0=u_rows[:, t, :], in1=hx_rows[:, t, :], op=ALU.mult)
+        def gate_state(engine, t):
+            engine.tensor_tensor(out=u_hx[:, t, :], in0=u_rows[:, t, :], in1=hx_rows[:, t, :], op=ALU.mult)
 
-        def mix_block(accs, b, i, first, last):
-            for a in range(HID_TILES):
-                mx_pass(accs[a][:], w_mx[i], slice(a * P, (a + 1) * P), h_mx[b][i], slice(0, NODES), first, last)
+        def mix_tile(acc, b, i, a, first, last):
+            mx_pass(acc[:], w_mx[i], slice(a * P, (a + 1) * P), h_mx[b][i], slice(0, NODES), first, last)
 
         def candidate(acc, a):
             cand = gate.tile([P, NODES], F32, name="cand")
@@ -204,10 +213,12 @@ def tile_dcgrucell_pc_kernel(
             )
             return minus
 
-        def blend_and_store(t, minus):
+        def blend_and_store(t, minus, pieces=1):
             result = gate.tile([P, NODES], F32, name="result")
-            nc.vector.tensor_tensor(out=result[:], in0=u_hx[:, t, :], in1=minus[:], op=ALU.subtract)
-            nc.sync.dma_start(out=out_tiles[t], in_=result[:])
+            for k in range(pieces):
+                part = slice(k * NODES // pieces, (k + 1) * NODES // pieces)
+                nc.vector.tensor_tensor(out=result[:, part], in0=u_hx[:, t, part], in1=minus[:, part], op=ALU.subtract)
+                nc.sync.dma_start(out=out_tiles[t][:, part], in_=result[:, part])
 
         whole = (NODES,)
         halves = (NODES // 2, NODES // 2)
@@ -224,8 +235,9 @@ def tile_dcgrucell_pc_kernel(
         quantise(flip_x1, x1_mx[0][0], whole)
         quantise(flip_s0, s_mx[0], halves)
         near_x0_0 = side_tile()
-        channels_side_by_side(on_scalar, x0_rows[0], near_x0_0, 0, NODES // 2)
+        channels_side_by_side(on_vector, x0_rows[0], near_x0_0, 0, NODES // 2)
         x2 = diffusion_step(0, 0)
+        channels_side_by_side(on_vector, x0_rows[0], near_x0_0, NODES // 2, NODES)
         flip_s1 = nodes_to_partitions(s_rows[1])
         flip_x1 = nodes_to_partitions(x1_rows[1][0])
         flip_x1_0 = nodes_to_partitions(x1_rows[0][1])
@@ -233,63 +245,66 @@ def tile_dcgrucell_pc_kernel(
         quantise(flip_s1, s_mx[1], whole)
         quantise(x2, h_mx[0][X2[0]], whole)
         quantise(flip_x1, x1_mx[1][0], whole)
+        quantise(near_x0_0, h_mx[0][X0], whole)
         quantise(flip_x1_0, x1_mx[0][1], whole)
         quantise(flip_x1_1, x1_mx[1][1], whole)
-        for t in range(BATCH * HID_TILES):
-            gate_state(t)
-        channels_side_by_side(on_scalar, x0_rows[0], near_x0_0, NODES // 2, NODES)
+        for t in range(EARLY_GATES):
+            gate_state(nc.gpsimd, t)
+        near_x1 = side_tile()
         near_x1_1 = side_tile()
         near_x0 = side_tile()
         near_x1_0 = side_tile()
-        near_x1 = side_tile()
-        for half in range(2):
-            channels_through_tensor(x1_rows[1][0], near_x1, half)
         near_w = [None] * BLOCKS
 
-        def regroup_w(i):
+        def regroup_w(i, pieces=1):
             near_w[i] = side_tile(HID, w_side)
-            channels_side_by_side(on_scalar, w_rows[i], near_w[i], 0, HID)
+            for k in range(pieces):
+                channels_side_by_side(on_scalar, w_rows[i], near_w[i], k * HID // pieces, (k + 1) * HID // pieces)
 
         x2_10 = diffusion_step(1, 0)
-        channels_through_tensor(x1_rows[1][1], near_x1_1, 0)
-        regroup_w(MIX_ORDER[0])
+        channels_side_by_side(on_scalar, x1_rows[1][0], near_x1, 0, NODES)
+        channels_through_tensor(x1_rows[0][1], near_x1_0, 0)
+        channels_side_by_side(on_scalar, x1_rows[1][1], near_x1_1, 0, NODES)
         x2_01 = diffusion_step(0, 1)
-        channels_through_tensor(x1_rows[1][1], near_x1_1, 1)
-        regroup_w(MIX_ORDER[1])
+        regroup_w(MIX_ORDER[0])
+        channels_through_tensor(x1_rows[0][1], near_x1_0, 1)
         x2_11 = diffusion_step(1, 1)
-        for half in range(2):
-            channels_through_tensor(x0_rows[1], near_x0, half)
+        regroup_w(MIX_ORDER[1])
         regroup_w(MIX_ORDER[2])
         regroup_w(MIX_ORDER[3])
-        for half in range(2):
-            channels_through_tensor(x1_rows[0][1], near_x1_0, half)
-        regroup_w(MIX_ORDER[4])
+        regroup_w(MIX_ORDER[4], HID_TILES)
         quantise(x2_10, h_mx[0][X2[1]], whole)
         quantise(near_w[X2[0]], w_mx[X2[0]], w_widths)
         quantise(x2_01, h_mx[1][X2[0]], whole)
-        quantise(near_w[X2[1]], w_mx[X2[1]], w_widths)
         quantise(x2_11, h_mx[1][X2[1]], whole)
+        quantise(near_w[X2[1]], w_mx[X2[1]], w_widths)
         quantise(near_x1, h_mx[0][X1[1]], whole)
-        quantise(near_w[X1[1]], w_mx[X1[1]], w_widths)
-        quantise(near_x0_0, h_mx[0][X0], whole)
-        quantise(near_w[X0], w_mx[X0], w_widths)
         quantise(near_x1_1, h_mx[1][X1[1]], whole)
-        quantise(near_w[X1[0]], w_mx[X1[0]], w_widths)
+        quantise(near_w[X1[1]], w_mx[X1[1]], w_widths)
+        quantise(near_x1_0, h_mx[1][X1[0]], whole)
+        quantise(near_w[X0], w_mx[X0], w_widths)
+        channels_side_by_side(on_vector, x0_rows[1], near_x0, 0, NODES)
+        quantise(near_w[X1[0]], w_mx[X1[0]], HID_TILES * (P,))
+        quantise(near_x0, h_mx[1][X0], whole)
         accs = [
             [psum.tile([P, NODES], F32, name="mix_acc", tag="bank") for a in range(HID_TILES)]
             for b in range(BATCH)
         ]
-        for i in MIX_ORDER:
-            mix_block(accs[0], 0, i, i == MIX_ORDER[0], i == MIX_ORDER[-1])
-            if i in X2:
-                mix_block(accs[1], 1, i, i == MIX_ORDER[0], False)
-        quantise(near_x0, h_mx[1][X0], whole)
-        quantise(near_x1_0, h_mx[1][X1[0]], whole)
-        for i in MIX_ORDER[GRAPHS:]:
-            mix_block(accs[1], 1, i, False, i == MIX_ORDER[-1])
-        cands = [candidate(accs[b][a], a) for b in range(BATCH) for a in range(HID_TILES)]
-        minus = [gate_candidate(0, cands[0])]
-        for t in range(1, BATCH * HID_TILES):
-            minus.append(gate_candidate(t, cands[t]))
-            blend_and_store(t - 1, minus[t - 1])
-        blend_and_store(BATCH * HID_TILES - 1, minus[-1])
+        for i in MIX_ORDER[:3]:
+            for b in range(BATCH):
+                for a in range(HID_TILES):
+                    mix_tile(accs[b][a], b, i, a, i == MIX_ORDER[0], False)
+        for b in range(BATCH):
+            for a in range(HID_TILES):
+                for i in MIX_ORDER[3:]:
+                    mix_tile(accs[b][a], b, i, a, False, i == MIX_ORDER[-1])
+        for t in range(EARLY_GATES, BATCH * HID_TILES):
+            gate_state(nc.vector, t)
+        order = [(b, a) for b in range(BATCH) for a in range(HID_TILES)]
+        cands = [candidate(accs[b][a], a) for b, a in order]
+        tiles = [b * HID_TILES + a for b, a in order]
+        minus = [gate_candidate(tiles[0], cands[0])]
+        for k in range(1, BATCH * HID_TILES):
+            minus.append(gate_candidate(tiles[k], cands[k]))
+            blend_and_store(tiles[k - 1], minus[k - 1])
+        blend_and_store(tiles[-1], minus[-1], 2)

@@ -22,9 +22,8 @@ HID_TILES = HID // P
 BLOCKS = 5
 X0, X1, X2 = 0, (1, 3), (2, 4)
 MIX_ORDER = (X2[0], X2[1], X1[1], X0, X1[0])
-EARLY_GATES = 5
 PSUM_BANKS = 8
-SIDE_BUFS = 14
+SIDE_BUFS = 13
 
 FLOPS = 2 * GRAPHS * BATCH * CH * NODES * NODES + 2 * BATCH * BLOCKS * CH * HID * NODES
 
@@ -37,9 +36,9 @@ def tile_dcgrucell_pc_kernel(
         const = ctx.enter_context(tc.tile_pool(name="const", bufs=1))
         raw = ctx.enter_context(tc.tile_pool(name="raw", bufs=1))
         side = ctx.enter_context(tc.tile_pool(name="side", bufs=SIDE_BUFS))
-        w_side = ctx.enter_context(tc.tile_pool(name="w_side", bufs=BLOCKS))
+        wide = ctx.enter_context(tc.tile_pool(name="wide", bufs=1))
         mx = ctx.enter_context(tc.tile_pool(name="mx", bufs=1))
-        gate = ctx.enter_context(tc.tile_pool(name="gate", bufs=BATCH * HID_TILES))
+        gate = ctx.enter_context(tc.tile_pool(name="gate", bufs=1))
         psum = ctx.enter_context(tc.psum_pool(name="psum", bufs=PSUM_BANKS))
         ctx.enter_context(tc.manual_schedule())
 
@@ -79,9 +78,9 @@ def tile_dcgrucell_pc_kernel(
             nc.sync.dma_start(out=hx_rows[:, first:end, :], in_=hx_tiles[:, first:end, :])
             nc.sync.dma_start(out=u_rows[:, first:end, :], in_=u_tiles[:, first:end, :])
 
-        load_gate(0, EARLY_GATES - 1)
+        load_gate(0, 4)
         x0_rows[1] = load_channels(x_cand, 1, "x0_rows1", 1)
-        load_gate(EARLY_GATES - 1, EARLY_GATES)
+        load_gate(4, BATCH * HID_TILES)
         w_rows = [None] * BLOCKS
         for i in MIX_ORDER:
             w_rows[i] = raw.tile([P, PACK * HID], BF16, name="w_rows%d" % i)
@@ -89,7 +88,6 @@ def tile_dcgrucell_pc_kernel(
                 out=w_rows[i][:],
                 in_=W_c[i * CH : (i + 1) * CH, :].rearrange("(p j) o -> p (j o)", j=PACK),
             )
-        load_gate(EARLY_GATES, BATCH * HID_TILES)
 
         ident = const.tile([P, P], F32, name="ident")
         make_identity(nc, ident[:])
@@ -132,8 +130,22 @@ def tile_dcgrucell_pc_kernel(
 
         s_mx = [mx_operand(NODES, "s_mx%d" % g) for g in range(GRAPHS)]
         x1_mx = [[mx_operand(CH, "x1_mx%d%d" % (g, b)) for b in range(BATCH)] for g in range(GRAPHS)]
-        h_mx = [[mx_operand(NODES, "h_mx%d%d" % (b, i)) for i in range(BLOCKS)] for b in range(BATCH)]
-        w_mx = [mx_operand(HID, "w_mx%d" % i) for i in range(BLOCKS)]
+        def part_of(operand, first, width):
+            return operand[0][:, first : first + width], operand[1][:, first : first + width]
+
+        h_mx = [[None] * BLOCKS for b in range(BATCH)]
+        for b, i in ((0, X1[0]), (0, X0), (0, X2[0]), (0, X2[1]), (1, X1[0]), (1, X0)):
+            h_mx[b][i] = mx_operand(NODES, "h_mx%d%d" % (b, i))
+        x2_mx = mx_operand(2 * NODES, "x2_mx")
+        h_mx[1][X2[0]], h_mx[1][X2[1]] = part_of(x2_mx, 0, NODES), part_of(x2_mx, NODES, NODES)
+        x11_mx = mx_operand(2 * NODES, "x11_mx")
+        h_mx[0][X1[1]], h_mx[1][X1[1]] = part_of(x11_mx, 0, NODES), part_of(x11_mx, NODES, NODES)
+        w_pairs = [mx_operand(2 * HID, "w_mx%d" % k) for k in range(2)]
+        w_mx = [None] * BLOCKS
+        w_mx[MIX_ORDER[0]] = mx_operand(HID, "w_mx_first")
+        for k in range(2):
+            for e in range(2):
+                w_mx[MIX_ORDER[1 + 2 * k + e]] = part_of(w_pairs[k], e * HID, HID)
 
         def nodes_to_partitions(rows):
             words = rows[:].bitcast(F32).rearrange("p (s w) -> p s w", s=PACK)
@@ -154,12 +166,13 @@ def tile_dcgrucell_pc_kernel(
                 )
             return packed
 
-        def side_tile(width=NODES, pool=side):
-            packed = pool.tile([P, width * PACK], BF16, name="packed", tag="side", align_bytes=64)
+        def side_tile(width=NODES, name="side"):
+            pool = side if name == "side" else wide
+            packed = pool.tile([P, width * PACK], BF16, name=name, tag=name, align_bytes=64)
             return packed
 
         def channels_side_by_side(copy, rows, packed, first, end):
-            to = packed[:].rearrange("p (c i j) -> p c j i", i=4, j=PACK)
+            to = packed.rearrange("p (c i j) -> p c j i", i=4, j=PACK)
             frm = rows[:].rearrange("p (j c i) -> p c j i", j=PACK, i=4)
             copy(out=to[:, first // 4 : end // 4], in_=frm[:, first // 4 : end // 4])
 
@@ -173,9 +186,8 @@ def tile_dcgrucell_pc_kernel(
                 nc.tensor.matmul(out=to[:, part, :], lhsT=ident_bf[:], rhs=frm[:, part, :], start=True, stop=True)
             nc.scalar.copy(out=packed[:, half * nodes * PACK : (half + 1) * nodes * PACK], in_=bank[:])
 
-        def diffusion_step(g, b):
-            packed = side.tile([P, NODES * PACK], BF16, name="packed", tag="side", align_bytes=64)
-            packed_nj = packed[:].rearrange("p (n j) -> p n j", j=PACK)
+        def diffusion_step(g, b, packed):
+            packed_nj = packed.rearrange("p (n j) -> p n j", j=PACK)
             x0_jn = x0_rows[b][:].rearrange("p (j n) -> p j n", j=PACK)
             for r in range(NODES // P):
                 nodes = slice(r * P, (r + 1) * P)
@@ -193,51 +205,42 @@ def tile_dcgrucell_pc_kernel(
             return packed
 
         u_hx = const.tile([P, BATCH * HID_TILES, NODES], F32, name="u_hx")
-        out_tiles = out.rearrange("b (a p) n -> (b a) p n", p=P)
+        out_tiles = out.rearrange("b (a p) n -> p (b a) n", p=P)
 
-        def gate_state(engine, t):
-            engine.tensor_tensor(out=u_hx[:, t, :], in0=u_rows[:, t, :], in1=hx_rows[:, t, :], op=ALU.mult)
+        def gate_state(t):
+            nc.gpsimd.tensor_tensor(out=u_hx[:, t, :], in0=u_rows[:, t, :], in1=hx_rows[:, t, :], op=ALU.mult)
 
         def mix_tile(acc, b, i, a, first, last):
             mx_pass(acc[:], w_mx[i], slice(a * P, (a + 1) * P), h_mx[b][i], slice(0, NODES), first, last)
 
-        def candidate(acc, a):
-            cand = gate.tile([P, NODES], F32, name="cand")
-            nc.scalar.activation(out=cand[:], in_=acc[:], func=ACT.Tanh, bias=bias[:, a : a + 1], scale=1.0)
-            return cand
+        def candidate(acc, a, cand):
+            nc.scalar.activation(out=cand, in_=acc[:], func=ACT.Tanh, bias=bias[:, a : a + 1], scale=1.0)
 
-        def gate_candidate(t, cand):
-            minus = gate.tile([P, NODES], F32, name="minus")
+        def gate_candidate(first, end, cand):
             nc.vector.scalar_tensor_tensor(
-                out=minus[:], in0=u_rows[:, t, :], scalar=1.0, in1=cand[:], op0=ALU.subtract, op1=ALU.mult
+                out=cand, in0=u_rows[:, first:end, :], scalar=1.0, in1=cand, op0=ALU.subtract, op1=ALU.mult
             )
-            return minus
 
-        def blend_and_store(t, minus, pieces=1):
-            result = gate.tile([P, NODES], F32, name="result")
-            for k in range(pieces):
-                part = slice(k * NODES // pieces, (k + 1) * NODES // pieces)
-                nc.vector.tensor_tensor(out=result[:, part], in0=u_hx[:, t, part], in1=minus[:, part], op=ALU.subtract)
-                nc.sync.dma_start(out=out_tiles[t][:, part], in_=result[:, part])
+        def blend_and_store(first, end, cand):
+            nc.vector.tensor_tensor(out=cand, in0=u_hx[:, first:end, :], in1=cand, op=ALU.subtract)
+            nc.sync.dma_start(out=out_tiles[:, first:end, :], in_=cand)
 
         whole = (NODES,)
         halves = (NODES // 2, NODES // 2)
-        w_widths = (2 * P, P)
         on_scalar = nc.scalar.copy
         on_vector = nc.vector.tensor_copy
 
         flip_x1 = nodes_to_partitions(x1_rows[0][0])
         near_x1 = side_tile()
-        channels_side_by_side(on_vector, x1_rows[0][0], near_x1, 0, NODES // 2)
-        channels_side_by_side(on_vector, x1_rows[0][0], near_x1, NODES // 2, NODES)
+        channels_side_by_side(on_vector, x1_rows[0][0], near_x1[:], 0, NODES)
         quantise(near_x1, h_mx[0][X1[0]], whole)
         flip_s0 = nodes_to_partitions(s_rows[0])
         quantise(flip_x1, x1_mx[0][0], whole)
         quantise(flip_s0, s_mx[0], halves)
         near_x0_0 = side_tile()
-        channels_side_by_side(on_vector, x0_rows[0], near_x0_0, 0, NODES // 2)
-        x2 = diffusion_step(0, 0)
-        channels_side_by_side(on_vector, x0_rows[0], near_x0_0, NODES // 2, NODES)
+        channels_side_by_side(on_scalar, x0_rows[0], near_x0_0[:], 0, NODES)
+        x2 = side_tile()
+        diffusion_step(0, 0, x2[:])
         flip_s1 = nodes_to_partitions(s_rows[1])
         flip_x1 = nodes_to_partitions(x1_rows[1][0])
         flip_x1_0 = nodes_to_partitions(x1_rows[0][1])
@@ -248,63 +251,69 @@ def tile_dcgrucell_pc_kernel(
         quantise(near_x0_0, h_mx[0][X0], whole)
         quantise(flip_x1_0, x1_mx[0][1], whole)
         quantise(flip_x1_1, x1_mx[1][1], whole)
-        for t in range(EARLY_GATES):
-            gate_state(nc.gpsimd, t)
-        near_x1 = side_tile()
-        near_x1_1 = side_tile()
+        for t in range(BATCH * HID_TILES):
+            gate_state(t)
+        near_x11 = side_tile(2 * NODES, "near_x11")
+        near_x11_b = [near_x11[:, b * NODES * PACK : (b + 1) * NODES * PACK] for b in range(BATCH)]
+        x2_b1 = side_tile(2 * NODES, "x2_b1")
+        x2_b1_g = [x2_b1[:, g * NODES * PACK : (g + 1) * NODES * PACK] for g in range(GRAPHS)]
         near_x0 = side_tile()
         near_x1_0 = side_tile()
-        near_w = [None] * BLOCKS
+        near_w = [side_tile(HID, "near_w0"), side_tile(2 * HID, "near_w1"), side_tile(2 * HID, "near_w2")]
 
-        def regroup_w(i, pieces=1):
-            near_w[i] = side_tile(HID, w_side)
-            for k in range(pieces):
-                channels_side_by_side(on_scalar, w_rows[i], near_w[i], k * HID // pieces, (k + 1) * HID // pieces)
+        def regroup_w(k):
+            first = (k + 1) % 2 * HID * PACK if k > 0 else 0
+            packed = near_w[(k + 1) // 2][:, first : first + HID * PACK]
+            channels_side_by_side(on_scalar, w_rows[MIX_ORDER[k]], packed, 0, HID)
 
-        x2_10 = diffusion_step(1, 0)
-        channels_side_by_side(on_scalar, x1_rows[1][0], near_x1, 0, NODES)
+        x2_10 = side_tile()
+        diffusion_step(1, 0, x2_10[:])
+        channels_side_by_side(on_scalar, x1_rows[1][0], near_x11_b[0], 0, NODES)
         channels_through_tensor(x1_rows[0][1], near_x1_0, 0)
-        channels_side_by_side(on_scalar, x1_rows[1][1], near_x1_1, 0, NODES)
-        x2_01 = diffusion_step(0, 1)
-        regroup_w(MIX_ORDER[0])
+        channels_side_by_side(on_scalar, x1_rows[1][1], near_x11_b[1], 0, NODES)
+        diffusion_step(0, 1, x2_b1_g[0])
+        regroup_w(0)
         channels_through_tensor(x1_rows[0][1], near_x1_0, 1)
-        x2_11 = diffusion_step(1, 1)
-        regroup_w(MIX_ORDER[1])
-        regroup_w(MIX_ORDER[2])
-        regroup_w(MIX_ORDER[3])
-        regroup_w(MIX_ORDER[4], HID_TILES)
+        diffusion_step(1, 1, x2_b1_g[1])
+        for k in range(1, BLOCKS):
+            regroup_w(k)
+        for half in range(2):
+            channels_through_tensor(x0_rows[1], near_x0, half)
         quantise(x2_10, h_mx[0][X2[1]], whole)
-        quantise(near_w[X2[0]], w_mx[X2[0]], w_widths)
-        quantise(x2_01, h_mx[1][X2[0]], whole)
-        quantise(x2_11, h_mx[1][X2[1]], whole)
-        quantise(near_w[X2[1]], w_mx[X2[1]], w_widths)
-        quantise(near_x1, h_mx[0][X1[1]], whole)
-        quantise(near_x1_1, h_mx[1][X1[1]], whole)
-        quantise(near_w[X1[1]], w_mx[X1[1]], w_widths)
+        quantise(near_w[0], w_mx[MIX_ORDER[0]], (2 * P, P))
+        quantise(x2_b1, x2_mx, (2 * NODES,))
+        quantise(near_w[1], w_pairs[0], (NODES, 2 * P))
+        quantise(near_x11, x11_mx, (2 * NODES,))
+        quantise(near_w[2], w_pairs[1], (NODES, 2 * P))
         quantise(near_x1_0, h_mx[1][X1[0]], whole)
-        quantise(near_w[X0], w_mx[X0], w_widths)
-        channels_side_by_side(on_vector, x0_rows[1], near_x0, 0, NODES)
-        quantise(near_w[X1[0]], w_mx[X1[0]], HID_TILES * (P,))
         quantise(near_x0, h_mx[1][X0], whole)
         accs = [
             [psum.tile([P, NODES], F32, name="mix_acc", tag="bank") for a in range(HID_TILES)]
             for b in range(BATCH)
         ]
-        for i in MIX_ORDER[:3]:
-            for b in range(BATCH):
-                for a in range(HID_TILES):
-                    mix_tile(accs[b][a], b, i, a, i == MIX_ORDER[0], False)
+
+        def mix(b, blocks, tiles):
+            for i in blocks:
+                for a in tiles:
+                    mix_tile(accs[b][a], b, i, a, i == MIX_ORDER[0], i == MIX_ORDER[-1])
+
+        every = range(HID_TILES)
+        mix(0, MIX_ORDER[:1], every)
+        mix(1, MIX_ORDER[:1], every)
+        mix(0, MIX_ORDER[1:3], every)
+        for a in every:
+            mix(0, MIX_ORDER[3:], (a,))
+        for a in every:
+            mix(1, MIX_ORDER[1:], (a,))
+        groups = ((0, 1), (1, 2), (2, 3), (3, 5), (5, 6))
+        cands = gate.tile([P, BATCH * HID_TILES, NODES], F32, name="cands")
         for b in range(BATCH):
             for a in range(HID_TILES):
-                for i in MIX_ORDER[3:]:
-                    mix_tile(accs[b][a], b, i, a, False, i == MIX_ORDER[-1])
-        for t in range(EARLY_GATES, BATCH * HID_TILES):
-            gate_state(nc.vector, t)
-        order = [(b, a) for b in range(BATCH) for a in range(HID_TILES)]
-        cands = [candidate(accs[b][a], a) for b, a in order]
-        tiles = [b * HID_TILES + a for b, a in order]
-        minus = [gate_candidate(tiles[0], cands[0])]
-        for k in range(1, BATCH * HID_TILES):
-            minus.append(gate_candidate(tiles[k], cands[k]))
-            blend_and_store(tiles[k - 1], minus[k - 1])
-        blend_and_store(tiles[-1], minus[-1], 2)
+                candidate(accs[b][a], a, cands[:, b * HID_TILES + a, :])
+        for k, (first, end) in enumerate(groups):
+            gate_candidate(first, end, cands[:, first:end, :])
+            if k > 0:
+                first, end = groups[k - 1]
+                blend_and_store(first, end, cands[:, first:end, :])
+        first, end = groups[-1]
+        blend_and_store(first, end, cands[:, first:end, :])

@@ -66,8 +66,8 @@ def tile_dcgrucell_pc_kernel(
         x0_rows[0] = load_channels(x_cand, 0, "x0_rows0", 1)
         s_rows[1] = load_support(support1, "s_rows1")
         x1_rows[1][0] = load_channels(x1_1, 0, "x1_rows10", 2)
-        x1_rows[0][1] = load_channels(x1_0, 1, "x1_rows01", 2)
-        x1_rows[1][1] = load_channels(x1_1, 1, "x1_rows11", 2)
+        x1_rows[0][1] = load_channels(x1_0, 1, "x1_rows01", 1)
+        x1_rows[1][1] = load_channels(x1_1, 1, "x1_rows11", 1)
         hx_rows = raw.tile([P, BATCH * HID_TILES, NODES], BF16, name="hx_rows")
         u_rows = raw.tile([P, BATCH * HID_TILES, NODES], BF16, name="u_rows")
 
@@ -89,15 +89,14 @@ def tile_dcgrucell_pc_kernel(
                 in_=W_c[i * CH : (i + 1) * CH, :].rearrange("(p j) o -> p (j o)", j=PACK),
             )
 
+        bias = const.tile([P, HID_TILES], BF16, name="bias")
+        with nc.allow_non_contiguous_dma(reason="384 bias values, one to a partition and tile"):
+            nc.sync.dma_start(out=bias[:], in_=b_c.rearrange("(a p) -> p a", p=P))
+
         ident = const.tile([P, P], F32, name="ident")
         make_identity(nc, ident[:])
         ident_bf = const.tile([P, P], BF16, name="ident_bf")
         make_identity(nc, ident_bf[:])
-        bias_bf = const.tile([P, HID_TILES], BF16, name="bias_bf")
-        with nc.allow_non_contiguous_dma(reason="384 bias values, one to a partition and tile"):
-            nc.scalar.dma_start(out=bias_bf[:], in_=b_c.rearrange("(a p) -> p a", p=P))
-        bias = const.tile([P, HID_TILES], F32, name="bias")
-        nc.gpsimd.tensor_copy(out=bias[:], in_=bias_bf[:])
         warm = const.tile([P, 1], F32, name="warm")
         nc.scalar.activation(out=warm[:], in_=ident[:, 0:1], func=ACT.Tanh)
 
@@ -186,9 +185,8 @@ def tile_dcgrucell_pc_kernel(
                 nc.tensor.matmul(out=to[:, part, :], lhsT=ident_bf[:], rhs=frm[:, part, :], start=True, stop=True)
             nc.scalar.copy(out=packed[:, half * nodes * PACK : (half + 1) * nodes * PACK], in_=bank[:])
 
-        def diffusion_step(g, b, packed):
+        def diffusion_step(g, b, packed, x0_nj):
             packed_nj = packed.rearrange("p (n j) -> p n j", j=PACK)
-            x0_jn = x0_rows[b][:].rearrange("p (j n) -> p j n", j=PACK)
             for r in range(NODES // P):
                 nodes = slice(r * P, (r + 1) * P)
                 bank = psum.tile([P, PACK, P], F32, name="step_bank", tag="bank")
@@ -198,7 +196,7 @@ def tile_dcgrucell_pc_kernel(
                     out=packed_nj[:, nodes, :],
                     in0=bank[:].rearrange("p j n -> p n j"),
                     scalar=2.0,
-                    in1=x0_jn[:, :, nodes].rearrange("p j n -> p n j"),
+                    in1=x0_nj[:, nodes, :],
                     op0=ALU.mult,
                     op1=ALU.subtract,
                 )
@@ -240,7 +238,7 @@ def tile_dcgrucell_pc_kernel(
         near_x0_0 = side_tile()
         channels_side_by_side(on_scalar, x0_rows[0], near_x0_0[:], 0, NODES)
         x2 = side_tile()
-        diffusion_step(0, 0, x2[:])
+        diffusion_step(0, 0, x2[:], x0_rows[0][:].rearrange("p (j n) -> p n j", j=PACK))
         flip_s1 = nodes_to_partitions(s_rows[1])
         flip_x1 = nodes_to_partitions(x1_rows[1][0])
         flip_x1_0 = nodes_to_partitions(x1_rows[0][1])
@@ -267,14 +265,15 @@ def tile_dcgrucell_pc_kernel(
             channels_side_by_side(on_scalar, w_rows[MIX_ORDER[k]], packed, 0, HID)
 
         x2_10 = side_tile()
-        diffusion_step(1, 0, x2_10[:])
+        diffusion_step(1, 0, x2_10[:], near_x0_0[:].rearrange("p (n j) -> p n j", j=PACK))
         channels_side_by_side(on_scalar, x1_rows[1][0], near_x11_b[0], 0, NODES)
         channels_through_tensor(x1_rows[0][1], near_x1_0, 0)
         channels_side_by_side(on_scalar, x1_rows[1][1], near_x11_b[1], 0, NODES)
-        diffusion_step(0, 1, x2_b1_g[0])
+        x0_nj = x0_rows[1][:].rearrange("p (j n) -> p n j", j=PACK)
+        diffusion_step(0, 1, x2_b1_g[0], x0_nj)
         regroup_w(0)
         channels_through_tensor(x1_rows[0][1], near_x1_0, 1)
-        diffusion_step(1, 1, x2_b1_g[1])
+        diffusion_step(1, 1, x2_b1_g[1], x0_nj)
         for k in range(1, BLOCKS):
             regroup_w(k)
         for half in range(2):

@@ -55,16 +55,16 @@ def tile_dcgrucell_pc_kernel(
         def load_channels(x, b, name, pieces):
             return load_row_sets(x[b].rearrange("(p j) n -> p j n", j=PACK), name, pieces)
 
-        def load_support(support, name, pieces=2):
-            return load_row_sets(support.rearrange("(a p) n -> p a n", p=P), name, pieces)
+        def load_support(support, name, pattern, pieces=2):
+            return load_row_sets(support.rearrange(pattern, p=P), name, pieces)
 
         x0_rows = [None] * BATCH
         x1_rows = [[None] * BATCH for g in range(GRAPHS)]
         s_rows = [None] * GRAPHS
         x1_rows[0][0] = load_channels(x1_0, 0, "x1_rows00", 2)
-        s_rows[0] = load_support(support0, "s_rows0", 2)
+        s_rows[0] = load_support(support0, "s_rows0", "(a p) n -> p a n")
         x0_rows[0] = load_channels(x_cand, 0, "x0_rows0", 1)
-        s_rows[1] = load_support(support1, "s_rows1")
+        s_rows[1] = load_support(support1, "s_rows1", "(p a) n -> p a n")
         x1_rows[1][0] = load_channels(x1_1, 0, "x1_rows10", 2)
         x1_rows[0][1] = load_channels(x1_0, 1, "x1_rows01", 1)
         x1_rows[1][1] = load_channels(x1_1, 1, "x1_rows11", 1)
@@ -146,7 +146,7 @@ def tile_dcgrucell_pc_kernel(
             for e in range(2):
                 w_mx[MIX_ORDER[1 + 2 * k + e]] = part_of(w_pairs[k], e * HID, HID)
 
-        def nodes_to_partitions(rows):
+        def nodes_to_partitions(rows, adjacent=False):
             words = rows[:].bitcast(F32).rearrange("p (s w) -> p s w", s=PACK)
             packed = side.tile([P, PACK * CH], BF16, name="packed", tag="side", align_bytes=64)
             packed_words = packed[:].bitcast(F32).rearrange("p (c v) -> p c v", v=2)
@@ -159,6 +159,13 @@ def tile_dcgrucell_pc_kernel(
                             words[:, 2 * pair + s, v * P : (v + 1) * P],
                             ident[:],
                         )
+                if adjacent:
+                    to = packed[:].bitcast(F32).rearrange("p (q s v) -> p q s v", s=PACK, v=2)
+                    nc.scalar.copy(
+                        out=to[:, :, 2 * pair : 2 * pair + 2, :],
+                        in_=bank[:].rearrange("p v (s q) -> p q s v", s=2),
+                    )
+                    continue
                 nc.scalar.copy(
                     out=packed_words[:, pair * 2 * P : (pair + 1) * 2 * P, :],
                     in_=bank[:].rearrange("p v c -> p c v"),
@@ -239,7 +246,7 @@ def tile_dcgrucell_pc_kernel(
         channels_side_by_side(on_scalar, x0_rows[0], near_x0_0[:], 0, NODES)
         x2 = side_tile()
         diffusion_step(0, 0, x2[:], x0_rows[0][:].rearrange("p (j n) -> p n j", j=PACK))
-        flip_s1 = nodes_to_partitions(s_rows[1])
+        flip_s1 = nodes_to_partitions(s_rows[1], adjacent=True)
         flip_x1 = nodes_to_partitions(x1_rows[1][0])
         flip_x1_0 = nodes_to_partitions(x1_rows[0][1])
         flip_x1_1 = nodes_to_partitions(x1_rows[1][1])
@@ -259,10 +266,10 @@ def tile_dcgrucell_pc_kernel(
         near_x1_0 = side_tile()
         near_w = [side_tile(HID, "near_w0"), side_tile(2 * HID, "near_w1"), side_tile(2 * HID, "near_w2")]
 
-        def regroup_w(k):
+        def regroup_w(copy, k):
             first = (k + 1) % 2 * HID * PACK if k > 0 else 0
             packed = near_w[(k + 1) // 2][:, first : first + HID * PACK]
-            channels_side_by_side(on_scalar, w_rows[MIX_ORDER[k]], packed, 0, HID)
+            channels_side_by_side(copy, w_rows[MIX_ORDER[k]], packed, 0, HID)
 
         x2_10 = side_tile()
         diffusion_step(1, 0, x2_10[:], near_x0_0[:].rearrange("p (n j) -> p n j", j=PACK))
@@ -271,16 +278,18 @@ def tile_dcgrucell_pc_kernel(
         channels_side_by_side(on_scalar, x1_rows[1][1], near_x11_b[1], 0, NODES)
         x0_nj = x0_rows[1][:].rearrange("p (j n) -> p n j", j=PACK)
         diffusion_step(0, 1, x2_b1_g[0], x0_nj)
-        regroup_w(0)
+        regroup_w(on_scalar, 0)
         channels_through_tensor(x1_rows[0][1], near_x1_0, 1)
         diffusion_step(1, 1, x2_b1_g[1], x0_nj)
-        for k in range(1, BLOCKS):
-            regroup_w(k)
+        regroup_w(on_scalar, 1)
+        regroup_w(on_scalar, 3)
+        regroup_w(on_scalar, 4)
         for half in range(2):
             channels_through_tensor(x0_rows[1], near_x0, half)
         quantise(x2_10, h_mx[0][X2[1]], whole)
         quantise(near_w[0], w_mx[MIX_ORDER[0]], (2 * P, P))
         quantise(x2_b1, x2_mx, (2 * NODES,))
+        regroup_w(on_vector, 2)
         quantise(near_w[1], w_pairs[0], (NODES, 2 * P))
         quantise(near_x11, x11_mx, (2 * NODES,))
         quantise(near_w[2], w_pairs[1], (NODES, 2 * P))
@@ -304,7 +313,7 @@ def tile_dcgrucell_pc_kernel(
             mix(0, MIX_ORDER[3:], (a,))
         for a in every:
             mix(1, MIX_ORDER[1:], (a,))
-        groups = ((0, 1), (1, 2), (2, 3), (3, 5), (5, 6))
+        groups = ((0, 1), (1, 2), (2, 3), (3, 4), (4, 5), (5, 6))
         cands = gate.tile([P, BATCH * HID_TILES, NODES], F32, name="cands")
         for b in range(BATCH):
             for a in range(HID_TILES):

@@ -274,18 +274,18 @@ def tile_dcgrucell_pc_kernel(
         x2_10 = side_tile()
         diffusion_step(1, 0, x2_10[:], near_x0_0[:].rearrange("p (n j) -> p n j", j=PACK))
         channels_side_by_side(on_scalar, x1_rows[1][0], near_x11_b[0], 0, NODES)
-        channels_through_tensor(x1_rows[0][1], near_x1_0, 0)
         channels_side_by_side(on_scalar, x1_rows[1][1], near_x11_b[1], 0, NODES)
         x0_nj = x0_rows[1][:].rearrange("p (j n) -> p n j", j=PACK)
         diffusion_step(0, 1, x2_b1_g[0], x0_nj)
+        for half in range(2):
+            channels_through_tensor(x0_rows[1], near_x0, half)
         regroup_w(on_scalar, 0)
-        channels_through_tensor(x1_rows[0][1], near_x1_0, 1)
-        diffusion_step(1, 1, x2_b1_g[1], x0_nj)
+        diffusion_step(1, 1, x2_b1_g[1], near_x0[:].rearrange("p (n j) -> p n j", j=PACK))
         regroup_w(on_scalar, 1)
         regroup_w(on_scalar, 3)
         regroup_w(on_scalar, 4)
         for half in range(2):
-            channels_through_tensor(x0_rows[1], near_x0, half)
+            channels_through_tensor(x1_rows[0][1], near_x1_0, half)
         quantise(x2_10, h_mx[0][X2[1]], whole)
         quantise(near_w[0], w_mx[MIX_ORDER[0]], (2 * P, P))
         quantise(x2_b1, x2_mx, (2 * NODES,))
@@ -293,8 +293,8 @@ def tile_dcgrucell_pc_kernel(
         quantise(near_w[1], w_pairs[0], (NODES, 2 * P))
         quantise(near_x11, x11_mx, (2 * NODES,))
         quantise(near_w[2], w_pairs[1], (NODES, 2 * P))
-        quantise(near_x1_0, h_mx[1][X1[0]], whole)
         quantise(near_x0, h_mx[1][X0], whole)
+        quantise(near_x1_0, h_mx[1][X1[0]], whole)
         accs = [
             [psum.tile([P, NODES], F32, name="mix_acc", tag="bank") for a in range(HID_TILES)]
             for b in range(BATCH)

@@ -78,9 +78,9 @@ def tile_dcgrucell_pc_kernel(
             nc.sync.dma_start(out=hx_rows[:, first:end, :], in_=hx_tiles[:, first:end, :])
             nc.sync.dma_start(out=u_rows[:, first:end, :], in_=u_tiles[:, first:end, :])
 
-        load_gate(0, 4)
+        load_gate(0, 3)
         x0_rows[1] = load_channels(x_cand, 1, "x0_rows1", 1)
-        load_gate(4, BATCH * HID_TILES)
+        load_gate(3, 5)
         w_rows = [None] * BLOCKS
         for i in MIX_ORDER:
             w_rows[i] = raw.tile([P, PACK * HID], BF16, name="w_rows%d" % i)
@@ -89,6 +89,7 @@ def tile_dcgrucell_pc_kernel(
                 in_=W_c[i * CH : (i + 1) * CH, :].rearrange("(p j) o -> p (j o)", j=PACK),
             )
 
+        load_gate(5, 6)
         bias = const.tile([P, HID_TILES], BF16, name="bias")
         with nc.allow_non_contiguous_dma(reason="384 bias values, one to a partition and tile"):
             nc.sync.dma_start(out=bias[:], in_=b_c.rearrange("(a p) -> p a", p=P))
@@ -105,9 +106,8 @@ def tile_dcgrucell_pc_kernel(
             scales = mx.tile([P, width], U8, name=name + "_scales", align_bytes=64)
             return codes, scales
 
-        def quantise(packed, operand, widths):
+        def quantise(packed, operand, widths, first=0):
             codes, scales = operand
-            first = 0
             for w in widths:
                 nc.vector.quantize_mx(
                     out=codes[:, first : first + w].bitcast(FP8X4),
@@ -212,8 +212,8 @@ def tile_dcgrucell_pc_kernel(
         u_hx = const.tile([P, BATCH * HID_TILES, NODES], F32, name="u_hx")
         out_tiles = out.rearrange("b (a p) n -> p (b a) n", p=P)
 
-        def gate_state(t):
-            nc.gpsimd.tensor_tensor(out=u_hx[:, t, :], in0=u_rows[:, t, :], in1=hx_rows[:, t, :], op=ALU.mult)
+        def gate_state(engine, t):
+            engine.tensor_tensor(out=u_hx[:, t, :], in0=u_rows[:, t, :], in1=hx_rows[:, t, :], op=ALU.mult)
 
         def mix_tile(acc, b, i, a, first, last):
             mx_pass(acc[:], w_mx[i], slice(a * P, (a + 1) * P), h_mx[b][i], slice(0, NODES), first, last)
@@ -241,11 +241,14 @@ def tile_dcgrucell_pc_kernel(
         quantise(near_x1, h_mx[0][X1[0]], whole)
         flip_s0 = nodes_to_partitions(s_rows[0])
         quantise(flip_x1, x1_mx[0][0], whole)
-        quantise(flip_s0, s_mx[0], halves)
         near_x0_0 = side_tile()
-        channels_side_by_side(on_scalar, x0_rows[0], near_x0_0[:], 0, NODES)
+        x0_nj = near_x0_0[:].rearrange("p (n j) -> p n j", j=PACK)
+        quantise(flip_s0, s_mx[0], halves[:1])
+        channels_side_by_side(on_vector, x0_rows[0], near_x0_0[:], 0, NODES // 2)
+        channels_side_by_side(on_scalar, x0_rows[0], near_x0_0[:], NODES // 2, NODES)
+        quantise(flip_s0, s_mx[0], halves[1:], NODES // 2)
         x2 = side_tile()
-        diffusion_step(0, 0, x2[:], x0_rows[0][:].rearrange("p (j n) -> p n j", j=PACK))
+        diffusion_step(0, 0, x2[:], x0_nj)
         flip_s1 = nodes_to_partitions(s_rows[1], adjacent=True)
         flip_x1 = nodes_to_partitions(x1_rows[1][0])
         flip_x1_0 = nodes_to_partitions(x1_rows[0][1])
@@ -256,8 +259,10 @@ def tile_dcgrucell_pc_kernel(
         quantise(near_x0_0, h_mx[0][X0], whole)
         quantise(flip_x1_0, x1_mx[0][1], whole)
         quantise(flip_x1_1, x1_mx[1][1], whole)
-        for t in range(BATCH * HID_TILES):
-            gate_state(t)
+        waited = const.tile([P, 1], U32, name="waited")
+        nc.gpsimd.tensor_copy(out=waited[:], in_=x1_mx[1][1][0][:, 0:1])
+        for t in range(5):
+            gate_state(nc.gpsimd, t)
         near_x11 = side_tile(2 * NODES, "near_x11")
         near_x11_b = [near_x11[:, b * NODES * PACK : (b + 1) * NODES * PACK] for b in range(BATCH)]
         x2_b1 = side_tile(2 * NODES, "x2_b1")
@@ -272,20 +277,22 @@ def tile_dcgrucell_pc_kernel(
             channels_side_by_side(copy, w_rows[MIX_ORDER[k]], packed, 0, HID)
 
         x2_10 = side_tile()
-        diffusion_step(1, 0, x2_10[:], near_x0_0[:].rearrange("p (n j) -> p n j", j=PACK))
-        channels_side_by_side(on_scalar, x1_rows[1][0], near_x11_b[0], 0, NODES)
-        channels_side_by_side(on_scalar, x1_rows[1][1], near_x11_b[1], 0, NODES)
-        x0_nj = x0_rows[1][:].rearrange("p (j n) -> p n j", j=PACK)
-        diffusion_step(0, 1, x2_b1_g[0], x0_nj)
+        diffusion_step(1, 0, x2_10[:], x0_nj)
+        channels_side_by_side(on_scalar, x1_rows[1][0], near_x11_b[0], 0 * NODES // 2, 1 * NODES // 2)
         for half in range(2):
-            channels_through_tensor(x0_rows[1], near_x0, half)
+            channels_side_by_side(on_scalar, x0_rows[1], near_x0[:], half * NODES // 2, (half + 1) * NODES // 2)
+        x0_nj = near_x0[:].rearrange("p (n j) -> p n j", j=PACK)
+        channels_side_by_side(on_scalar, x1_rows[1][0], near_x11_b[0], 1 * NODES // 2, 2 * NODES // 2)
+        diffusion_step(0, 1, x2_b1_g[0], x0_nj)
+        channels_through_tensor(x1_rows[1][1], near_x11_b[1], 0)
+        channels_through_tensor(x1_rows[1][1], near_x11_b[1], 1)
         regroup_w(on_scalar, 0)
-        diffusion_step(1, 1, x2_b1_g[1], near_x0[:].rearrange("p (n j) -> p n j", j=PACK))
+        diffusion_step(1, 1, x2_b1_g[1], x0_nj)
         regroup_w(on_scalar, 1)
         regroup_w(on_scalar, 3)
         regroup_w(on_scalar, 4)
-        for half in range(2):
-            channels_through_tensor(x1_rows[0][1], near_x1_0, half)
+        channels_through_tensor(x1_rows[0][1], near_x1_0, 0)
+        channels_through_tensor(x1_rows[0][1], near_x1_0, 1)
         quantise(x2_10, h_mx[0][X2[1]], whole)
         quantise(near_w[0], w_mx[MIX_ORDER[0]], (2 * P, P))
         quantise(x2_b1, x2_mx, (2 * NODES,))
@@ -313,6 +320,8 @@ def tile_dcgrucell_pc_kernel(
             mix(0, MIX_ORDER[3:], (a,))
         for a in every:
             mix(1, MIX_ORDER[1:], (a,))
+        for t in range(5, BATCH * HID_TILES):
+            gate_state(nc.vector, t)
         groups = ((0, 1), (1, 2), (2, 3), (3, 4), (4, 5), (5, 6))
         cands = gate.tile([P, BATCH * HID_TILES, NODES], F32, name="cands")
         for b in range(BATCH):

@@ -22,6 +22,7 @@ HID_TILES = HID // P
 BLOCKS = 5
 X0, X1, X2 = 0, (1, 3), (2, 4)
 MIX_ORDER = (X2[0], X2[1], X1[1], X0, X1[0])
+GPSIMD_COLS = 2304
 PSUM_BANKS = 8
 SIDE_BUFS = 13
 
@@ -212,8 +213,13 @@ def tile_dcgrucell_pc_kernel(
         u_hx = const.tile([P, BATCH * HID_TILES, NODES], F32, name="u_hx")
         out_tiles = out.rearrange("b (a p) n -> p (b a) n", p=P)
 
-        def gate_state(engine, t):
-            engine.tensor_tensor(out=u_hx[:, t, :], in0=u_rows[:, t, :], in1=hx_rows[:, t, :], op=ALU.mult)
+        u_hx_cols = u_hx[:].rearrange("p t n -> p (t n)")
+        u_cols = u_rows[:].rearrange("p t n -> p (t n)")
+        hx_cols = hx_rows[:].rearrange("p t n -> p (t n)")
+
+        def gate_state(engine, first, end):
+            cols = slice(first, end)
+            engine.tensor_tensor(out=u_hx_cols[:, cols], in0=u_cols[:, cols], in1=hx_cols[:, cols], op=ALU.mult)
 
         def mix_tile(acc, b, i, a, first, last):
             mx_pass(acc[:], w_mx[i], slice(a * P, (a + 1) * P), h_mx[b][i], slice(0, NODES), first, last)
@@ -261,8 +267,8 @@ def tile_dcgrucell_pc_kernel(
         quantise(flip_x1_1, x1_mx[1][1], whole)
         waited = const.tile([P, 1], U32, name="waited")
         nc.gpsimd.tensor_copy(out=waited[:], in_=x1_mx[1][1][0][:, 0:1])
-        for t in range(5):
-            gate_state(nc.gpsimd, t)
+        for first in range(0, GPSIMD_COLS, NODES):
+            gate_state(nc.gpsimd, first, min(first + NODES, GPSIMD_COLS))
         near_x11 = side_tile(2 * NODES, "near_x11")
         near_x11_b = [near_x11[:, b * NODES * PACK : (b + 1) * NODES * PACK] for b in range(BATCH)]
         x2_b1 = side_tile(2 * NODES, "x2_b1")
@@ -282,12 +288,12 @@ def tile_dcgrucell_pc_kernel(
         for half in range(2):
             channels_side_by_side(on_scalar, x0_rows[1], near_x0[:], half * NODES // 2, (half + 1) * NODES // 2)
         x0_nj = near_x0[:].rearrange("p (n j) -> p n j", j=PACK)
-        channels_side_by_side(on_scalar, x1_rows[1][0], near_x11_b[0], 1 * NODES // 2, 2 * NODES // 2)
         diffusion_step(0, 1, x2_b1_g[0], x0_nj)
+        channels_through_tensor(x1_rows[1][0], near_x11_b[0], 1)
         channels_through_tensor(x1_rows[1][1], near_x11_b[1], 0)
-        channels_through_tensor(x1_rows[1][1], near_x11_b[1], 1)
         regroup_w(on_scalar, 0)
         diffusion_step(1, 1, x2_b1_g[1], x0_nj)
+        channels_through_tensor(x1_rows[1][1], near_x11_b[1], 1)
         regroup_w(on_scalar, 1)
         regroup_w(on_scalar, 3)
         regroup_w(on_scalar, 4)
@@ -295,12 +301,12 @@ def tile_dcgrucell_pc_kernel(
         channels_through_tensor(x1_rows[0][1], near_x1_0, 1)
         quantise(x2_10, h_mx[0][X2[1]], whole)
         quantise(near_w[0], w_mx[MIX_ORDER[0]], (2 * P, P))
-        quantise(x2_b1, x2_mx, (2 * NODES,))
         regroup_w(on_vector, 2)
+        quantise(x2_b1, x2_mx, (2 * NODES,))
         quantise(near_w[1], w_pairs[0], (NODES, 2 * P))
         quantise(near_x11, x11_mx, (2 * NODES,))
-        quantise(near_w[2], w_pairs[1], (NODES, 2 * P))
         quantise(near_x0, h_mx[1][X0], whole)
+        quantise(near_w[2], w_pairs[1], (NODES, 2 * P))
         quantise(near_x1_0, h_mx[1][X1[0]], whole)
         accs = [
             [psum.tile([P, NODES], F32, name="mix_acc", tag="bank") for a in range(HID_TILES)]
@@ -320,8 +326,7 @@ def tile_dcgrucell_pc_kernel(
             mix(0, MIX_ORDER[3:], (a,))
         for a in every:
             mix(1, MIX_ORDER[1:], (a,))
-        for t in range(5, BATCH * HID_TILES):
-            gate_state(nc.vector, t)
+        gate_state(nc.vector, GPSIMD_COLS, BATCH * HID_TILES * NODES)
         groups = ((0, 1), (1, 2), (2, 3), (3, 4), (4, 5), (5, 6))
         cands = gate.tile([P, BATCH * HID_TILES, NODES], F32, name="cands")
         for b in range(BATCH):

from contextlib import ExitStack

import concourse.mybir as mybir
from concourse.masks import make_identity

BF16 = mybir.dt.bfloat16
F32 = mybir.dt.float32
U32 = mybir.dt.uint32
U8 = mybir.dt.uint8
FP8X4 = mybir.dt.float8_e4m3fn_x4
ALU = mybir.AluOpType
ACT = mybir.ActivationFunctionType

P = 128
PACK = 4
BATCH = 2
GRAPHS = 2
CH = 512
NODES = 512
HID = 384
HID_TILES = HID // P
BLOCKS = 5
X0, X1, X2 = 0, (1, 3), (2, 4)
MIX_ORDER = (X2[0], X2[1], X1[1], X0, X1[0])
GPSIMD_COLS = 2304
PSUM_BANKS = 8
SIDE_BUFS = 13

FLOPS = 2 * GRAPHS * BATCH * CH * NODES * NODES + 2 * BATCH * BLOCKS * CH * HID * NODES


def tile_dcgrucell_pc_kernel(
    tc, x_cand, x1_0, x1_1, support0, support1, W_c, b_c, u, hx, out
):
    nc = tc.nc
    with ExitStack() as ctx:
        const = ctx.enter_context(tc.tile_pool(name="const", bufs=1))
        raw = ctx.enter_context(tc.tile_pool(name="raw", bufs=1))
        side = ctx.enter_context(tc.tile_pool(name="side", bufs=SIDE_BUFS))
        wide = ctx.enter_context(tc.tile_pool(name="wide", bufs=1))
        mx = ctx.enter_context(tc.tile_pool(name="mx", bufs=1))
        gate = ctx.enter_context(tc.tile_pool(name="gate", bufs=1))
        psum = ctx.enter_context(tc.psum_pool(name="psum", bufs=PSUM_BANKS))
        ctx.enter_context(tc.manual_schedule())

        def load_row_sets(view, name, pieces):
            rows = raw.tile([P, PACK * NODES], BF16, name=name)
            rows_sn = rows[:].rearrange("p (s n) -> p s n", s=PACK)
            sets = PACK // pieces
            for k in range(pieces):
                nc.sync.dma_start(
                    out=rows_sn[:, k * sets : (k + 1) * sets, :], in_=view[:, k * sets : (k + 1) * sets, :]
                )
            return rows

        def load_channels(x, b, name, pieces):
            return load_row_sets(x[b].rearrange("(p j) n -> p j n", j=PACK), name, pieces)

        def load_support(support, name, pattern, pieces=2):
            return load_row_sets(support.rearrange(pattern, p=P), name, pieces)

        x0_rows = [None] * BATCH
        x1_rows = [[None] * BATCH for g in range(GRAPHS)]
        s_rows = [None] * GRAPHS
        x1_rows[0][0] = load_channels(x1_0, 0, "x1_rows00", 2)
        s_rows[0] = load_support(support0, "s_rows0", "(a p) n -> p a n")
        x0_rows[0] = load_channels(x_cand, 0, "x0_rows0", 1)
        s_rows[1] = load_support(support1, "s_rows1", "(p a) n -> p a n")
        x1_rows[1][0] = load_channels(x1_1, 0, "x1_rows10", 2)
        x1_rows[0][1] = load_channels(x1_0, 1, "x1_rows01", 1)
        x1_rows[1][1] = load_channels(x1_1, 1, "x1_rows11", 1)
        hx_rows = raw.tile([P, BATCH * HID_TILES, NODES], BF16, name="hx_rows")
        u_rows = raw.tile([P, BATCH * HID_TILES, NODES], BF16, name="u_rows")

        hx_tiles = hx.rearrange("b (a p) n -> p (b a) n", p=P)
        u_tiles = u.rearrange("b (a p) n -> p (b a) n", p=P)

        def load_gate(first, end):
            nc.sync.dma_start(out=hx_rows[:, first:end, :], in_=hx_tiles[:, first:end, :])
            nc.sync.dma_start(out=u_rows[:, first:end, :], in_=u_tiles[:, first:end, :])

        load_gate(0, 3)
        x0_rows[1] = load_channels(x_cand, 1, "x0_rows1", 1)
        load_gate(3, 5)
        w_rows = [None] * BLOCKS
        for i in MIX_ORDER:
            w_rows[i] = raw.tile([P, PACK * HID], BF16, name="w_rows%d" % i)
            nc.sync.dma_start(
                out=w_rows[i][:],
                in_=W_c[i * CH : (i + 1) * CH, :].rearrange("(p j) o -> p (j o)", j=PACK),
            )

        load_gate(5, 6)
        bias = const.tile([P, HID_TILES], BF16, name="bias")
        with nc.allow_non_contiguous_dma(reason="384 bias values, one to a partition and tile"):
            nc.sync.dma_start(out=bias[:], in_=b_c.rearrange("(a p) -> p a", p=P))

        ident = const.tile([P, P], F32, name="ident")
        make_identity(nc, ident[:])
        ident_bf = const.tile([P, P], BF16, name="ident_bf")
        make_identity(nc, ident_bf[:])
        warm = const.tile([P, 1], F32, name="warm")
        nc.scalar.activation(out=warm[:], in_=ident[:, 0:1], func=ACT.Tanh)

        def mx_operand(width, name):
            codes = mx.tile([P, width], U32, name=name + "_codes", align_bytes=64)
            scales = mx.tile([P, width], U8, name=name + "_scales", align_bytes=64)
            return codes, scales

        def quantise(packed, operand, widths, first=0):
            codes, scales = operand
            for w in widths:
                nc.vector.quantize_mx(
                    out=codes[:, first : first + w].bitcast(FP8X4),
                    scales=scales[:, first : first + w],
                    in_=packed[:, first * PACK : (first + w) * PACK],
                )
                first += w

        def mx_pass(acc, stationary, s_cols, moving, m_cols, start, stop):
            nc.tensor.matmul_mx(
                out=acc,
                lhsT=stationary[0][:, s_cols].bitcast(FP8X4),
                lhsT_scale=stationary[1][:, s_cols],
                rhs=moving[0][:, m_cols].bitcast(FP8X4),
                rhs_scale=moving[1][:, m_cols],
                start=start,
                stop=stop,
            )

        s_mx = [mx_operand(NODES, "s_mx%d" % g) for g in range(GRAPHS)]
        x1_mx = [[mx_operand(CH, "x1_mx%d%d" % (g, b)) for b in range(BATCH)] for g in range(GRAPHS)]
        def part_of(operand, first, width):
            return operand[0][:, first : first + width], operand[1][:, first : first + width]

        h_mx = [[None] * BLOCKS for b in range(BATCH)]
        for b, i in ((0, X1[0]), (0, X0), (0, X2[0]), (0, X2[1]), (1, X1[0]), (1, X0)):
            h_mx[b][i] = mx_operand(NODES, "h_mx%d%d" % (b, i))
        x2_mx = mx_operand(2 * NODES, "x2_mx")
        h_mx[1][X2[0]], h_mx[1][X2[1]] = part_of(x2_mx, 0, NODES), part_of(x2_mx, NODES, NODES)
        x11_mx = mx_operand(2 * NODES, "x11_mx")
        h_mx[0][X1[1]], h_mx[1][X1[1]] = part_of(x11_mx, 0, NODES), part_of(x11_mx, NODES, NODES)
        w_pairs = [mx_operand(2 * HID, "w_mx%d" % k) for k in range(2)]
        w_mx = [None] * BLOCKS
        w_mx[MIX_ORDER[0]] = mx_operand(HID, "w_mx_first")
        for k in range(2):
            for e in range(2):
                w_mx[MIX_ORDER[1 + 2 * k + e]] = part_of(w_pairs[k], e * HID, HID)

        def nodes_to_partitions(rows, adjacent=False):
            words = rows[:].bitcast(F32).rearrange("p (s w) -> p s w", s=PACK)
            packed = side.tile([P, PACK * CH], BF16, name="packed", tag="side", align_bytes=64)
            packed_words = packed[:].bitcast(F32).rearrange("p (c v) -> p c v", v=2)
            for pair in range(2):
                bank = psum.tile([P, 2, 2 * P], F32, name="flip_bank", tag="bank")
                for s in range(2):
                    for v in range(2):
                        nc.tensor.transpose(
                            bank[:, v, s * P : (s + 1) * P],
                            words[:, 2 * pair + s, v * P : (v + 1) * P],
                            ident[:],
                        )
                if adjacent:
                    to = packed[:].bitcast(F32).rearrange("p (q s v) -> p q s v", s=PACK, v=2)
                    nc.scalar.copy(
                        out=to[:, :, 2 * pair : 2 * pair + 2, :],
                        in_=bank[:].rearrange("p v (s q) -> p q s v", s=2),
                    )
                    continue
                nc.scalar.copy(
                    out=packed_words[:, pair * 2 * P : (pair + 1) * 2 * P, :],
                    in_=bank[:].rearrange("p v c -> p c v"),
                )
            return packed

        def side_tile(width=NODES, name="side"):
            pool = side if name == "side" else wide
            packed = pool.tile([P, width * PACK], BF16, name=name, tag=name, align_bytes=64)
            return packed

        def channels_side_by_side(copy, rows, packed, first, end):
            to = packed.rearrange("p (c i j) -> p c j i", i=4, j=PACK)
            frm = rows[:].rearrange("p (j c i) -> p c j i", j=PACK, i=4)
            copy(out=to[:, first // 4 : end // 4], in_=frm[:, first // 4 : end // 4])

        def channels_through_tensor(rows, packed, half):
            nodes = NODES // 2
            bank = psum.tile([P, nodes * PACK], BF16, name="side_bank", tag="bank")
            to = bank[:].rearrange("p (n j) -> p n j", j=PACK)
            frm = rows[:].rearrange("p (j n) -> p n j", j=PACK)[:, half * nodes : (half + 1) * nodes, :]
            for k in range(2):
                part = slice(k * nodes // 2, (k + 1) * nodes // 2)
                nc.tensor.matmul(out=to[:, part, :], lhsT=ident_bf[:], rhs=frm[:, part, :], start=True, stop=True)
            nc.scalar.copy(out=packed[:, half * nodes * PACK : (half + 1) * nodes * PACK], in_=bank[:])

        def diffusion_step(g, b, packed, x0_nj):
            packed_nj = packed.rearrange("p (n j) -> p n j", j=PACK)
            for r in range(NODES // P):
                nodes = slice(r * P, (r + 1) * P)
                bank = psum.tile([P, PACK, P], F32, name="step_bank", tag="bank")
                for j in range(PACK):
                    mx_pass(bank[:, j, :], x1_mx[g][b], slice(j * P, (j + 1) * P), s_mx[g], nodes, True, True)
                nc.vector.scalar_tensor_tensor(
                    out=packed_nj[:, nodes, :],
                    in0=bank[:].rearrange("p j n -> p n j"),
                    scalar=2.0,
                    in1=x0_nj[:, nodes, :],
                    op0=ALU.mult,
                    op1=ALU.subtract,
                )
            return packed

        u_hx = const.tile([P, BATCH * HID_TILES, NODES], F32, name="u_hx")
        out_tiles = out.rearrange("b (a p) n -> p (b a) n", p=P)

        u_hx_cols = u_hx[:].rearrange("p t n -> p (t n)")
        u_cols = u_rows[:].rearrange("p t n -> p (t n)")
        hx_cols = hx_rows[:].rearrange("p t n -> p (t n)")

        def gate_state(engine, first, end):
            cols = slice(first, end)
            engine.tensor_tensor(out=u_hx_cols[:, cols], in0=u_cols[:, cols], in1=hx_cols[:, cols], op=ALU.mult)

        def mix_tile(acc, b, i, a, first, last):
            mx_pass(acc[:], w_mx[i], slice(a * P, (a + 1) * P), h_mx[b][i], slice(0, NODES), first, last)

        def candidate(acc, a, cand):
            nc.scalar.activation(out=cand, in_=acc[:], func=ACT.Tanh, bias=bias[:, a : a + 1], scale=1.0)

        def gate_candidate(first, end, cand):
            nc.vector.scalar_tensor_tensor(
                out=cand, in0=u_rows[:, first:end, :], scalar=1.0, in1=cand, op0=ALU.subtract, op1=ALU.mult
            )

        def blend_and_store(first, end, cand):
            nc.vector.tensor_tensor(out=cand, in0=u_hx[:, first:end, :], in1=cand, op=ALU.subtract)
            nc.sync.dma_start(out=out_tiles[:, first:end, :], in_=cand)

        whole = (NODES,)
        halves = (NODES // 2, NODES // 2)
        on_scalar = nc.scalar.copy
        on_vector = nc.vector.tensor_copy

        flip_x1 = nodes_to_partitions(x1_rows[0][0])
        near_x1 = side_tile()
        channels_side_by_side(on_vector, x1_rows[0][0], near_x1[:], 0, NODES)
        quantise(near_x1, h_mx[0][X1[0]], whole)
        flip_s0 = nodes_to_partitions(s_rows[0])
        quantise(flip_x1, x1_mx[0][0], whole)
        near_x0_0 = side_tile()
        x0_nj = near_x0_0[:].rearrange("p (n j) -> p n j", j=PACK)
        quantise(flip_s0, s_mx[0], halves[:1])
        channels_side_by_side(on_vector, x0_rows[0], near_x0_0[:], 0, NODES // 2)
        channels_side_by_side(on_scalar, x0_rows[0], near_x0_0[:], NODES // 2, NODES)
        quantise(flip_s0, s_mx[0], halves[1:], NODES // 2)
        x2 = side_tile()
        diffusion_step(0, 0, x2[:], x0_nj)
        flip_s1 = nodes_to_partitions(s_rows[1], adjacent=True)
        flip_x1 = nodes_to_partitions(x1_rows[1][0])
        flip_x1_0 = nodes_to_partitions(x1_rows[0][1])
        flip_x1_1 = nodes_to_partitions(x1_rows[1][1])
        quantise(flip_s1, s_mx[1], whole)
        quantise(x2, h_mx[0][X2[0]], whole)
        quantise(flip_x1, x1_mx[1][0], whole)
        quantise(near_x0_0, h_mx[0][X0], whole)
        quantise(flip_x1_0, x1_mx[0][1], whole)
        quantise(flip_x1_1, x1_mx[1][1], whole)
        waited = const.tile([P, 1], U32, name="waited")
        nc.gpsimd.tensor_copy(out=waited[:], in_=x1_mx[1][1][0][:, 0:1])
        for first in range(0, GPSIMD_COLS, NODES):
            gate_state(nc.gpsimd, first, min(first + NODES, GPSIMD_COLS))
        near_x11 = side_tile(2 * NODES, "near_x11")
        near_x11_b = [near_x11[:, b * NODES * PACK : (b + 1) * NODES * PACK] for b in range(BATCH)]
        x2_b1 = side_tile(2 * NODES, "x2_b1")
        x2_b1_g = [x2_b1[:, g * NODES * PACK : (g + 1) * NODES * PACK] for g in range(GRAPHS)]
        near_x0 = side_tile()
        near_x1_0 = side_tile()
        near_w = [side_tile(HID, "near_w0"), side_tile(2 * HID, "near_w1"), side_tile(2 * HID, "near_w2")]

        def regroup_w(copy, k):
            first = (k + 1) % 2 * HID * PACK if k > 0 else 0
            packed = near_w[(k + 1) // 2][:, first : first + HID * PACK]
            channels_side_by_side(copy, w_rows[MIX_ORDER[k]], packed, 0, HID)

        x2_10 = side_tile()
        diffusion_step(1, 0, x2_10[:], x0_nj)
        channels_side_by_side(on_scalar, x1_rows[1][0], near_x11_b[0], 0 * NODES // 2, 1 * NODES // 2)
        for half in range(2):
            channels_side_by_side(on_scalar, x0_rows[1], near_x0[:], half * NODES // 2, (half + 1) * NODES // 2)
        x0_nj = near_x0[:].rearrange("p (n j) -> p n j", j=PACK)
        diffusion_step(0, 1, x2_b1_g[0], x0_nj)
        channels_through_tensor(x1_rows[1][0], near_x11_b[0], 1)
        channels_through_tensor(x1_rows[1][1], near_x11_b[1], 0)
        regroup_w(on_scalar, 0)
        diffusion_step(1, 1, x2_b1_g[1], x0_nj)
        channels_through_tensor(x1_rows[1][1], near_x11_b[1], 1)
        regroup_w(on_scalar, 1)
        regroup_w(on_scalar, 3)
        regroup_w(on_scalar, 4)
        channels_through_tensor(x1_rows[0][1], near_x1_0, 0)
        channels_through_tensor(x1_rows[0][1], near_x1_0, 1)
        quantise(x2_10, h_mx[0][X2[1]], whole)
        quantise(near_w[0], w_mx[MIX_ORDER[0]], (2 * P, P))
        regroup_w(on_vector, 2)
        quantise(x2_b1, x2_mx, (2 * NODES,))
        quantise(near_w[1], w_pairs[0], (NODES, 2 * P))
        quantise(near_x11, x11_mx, (2 * NODES,))
        quantise(near_x0, h_mx[1][X0], whole)
        quantise(near_w[2], w_pairs[1], (NODES, 2 * P))
        quantise(near_x1_0, h_mx[1][X1[0]], whole)
        accs = [
            [psum.tile([P, NODES], F32, name="mix_acc", tag="bank") for a in range(HID_TILES)]
            for b in range(BATCH)
        ]

        def mix(b, blocks, tiles):
            for i in blocks:
                for a in tiles:
                    mix_tile(accs[b][a], b, i, a, i == MIX_ORDER[0], i == MIX_ORDER[-1])

        every = range(HID_TILES)
        mix(0, MIX_ORDER[:1], every)
        mix(1, MIX_ORDER[:1], every)
        mix(0, MIX_ORDER[1:3], every)
        for a in every:
            mix(0, MIX_ORDER[3:], (a,))
        for a in every:
            mix(1, MIX_ORDER[1:], (a,))
        gate_state(nc.vector, GPSIMD_COLS, BATCH * HID_TILES * NODES)
        groups = ((0, 1), (1, 2), (2, 3), (3, 4), (4, 5), (5, 6))
        cands = gate.tile([P, BATCH * HID_TILES, NODES], F32, name="cands")
        for b in range(BATCH):
            for a in range(HID_TILES):
                candidate(accs[b][a], a, cands[:, b * HID_TILES + a, :])
        for k, (first, end) in enumerate(groups):
            gate_candidate(first, end, cands[:, first:end, :])
            if k > 0:
                first, end = groups[k - 1]
                blend_and_store(first, end, cands[:, first:end, :])
        first, end = groups[-1]
        blend_and_store(first, end, cands[:, first:end, :])
